import numpy as np
import ml_dtypes


def mxq(x, axis, fmt="e4m3"):
    dtype, down = {"e4m3": (ml_dtypes.float8_e4m3fn, 7), "e5m2": (ml_dtypes.float8_e5m2, 14)}[fmt]
    v = np.moveaxis(np.asarray(x, np.float32).astype(ml_dtypes.bfloat16).astype(np.float64), axis, -1)
    blocks = v.reshape(v.shape[:-1] + (-1, 32))
    amax = np.abs(blocks).max(-1, keepdims=True)
    byte = np.maximum(np.where(amax > 0, np.frexp(amax)[1] - 1 + 127, 0) - down, 1)
    scale = np.exp2(byte - 127.0)
    codes = (blocks / scale).astype(np.float32).astype(dtype).astype(np.float64)
    return np.moveaxis((codes * scale).reshape(v.shape), -1, axis)


WIDE = False


def mx_kscale(k):
    if not WIDE:
        return np.ones(k)
    levels = np.array([10, -10, 5, -5, 0])
    a = np.random.permutation(np.resize(levels, k // 512 * 4)).reshape(k // 512, 4)
    idx = np.arange(k)
    return np.exp2(a[idx // 512, idx % 128 // 32])


BF16 = ml_dtypes.bfloat16


def bf(x):
    return np.asarray(x, np.float32).astype(BF16)


def f64(x):
    return np.asarray(x).astype(np.float64)


B, L, D, C, H, DFF, TE = 8, 32, 1024, 512, 8, 2048, 1000
EPS = 1e-5
ZMAX, NT = 6.0, 120


def erf(v):
    z = np.minimum(np.abs(v), ZMAX)
    z2 = 2.0 * z * z
    t = z.copy()
    s = z.copy()
    for n in range(1, NT):
        t *= z2
        t /= 2 * n + 1
        s += t
    return np.sign(v) * 2.0 / np.sqrt(np.pi) * np.exp(-z * z) * s


def gelu(v):
    return 0.5 * v * (1.0 + erf(v / np.sqrt(2.0)))


def layer_norm(v, g, b):
    mu = v.mean(-1, keepdims=True)
    var = ((v - mu) ** 2).mean(-1, keepdims=True)
    return (v - mu) / np.sqrt(var + EPS) * g + b


def setup_inputs():
    r = np.random.standard_normal
    s = mx_kscale(D)
    s2 = np.concatenate([s, s])
    return {"x_attn": bf(r((B, L, D)) * s),
            "cw1": bf(r((2 * D, C)) * 0.7 / np.sqrt(D) / s2[:, None]),
            "cb1": bf(r(C) * 0.3),
            "cw2": bf(r((C, D)) / np.sqrt(C)),
            "cb2": bf(r(D) * 0.3),
            "cln_g": bf(1.0 + 0.2 * r(D)),
            "cln_b": bf(r(D) * 0.2)}


def reference(x_attn, cw1, cb1, cw2, cb2, cln_g, cln_b):
    xq = mxq(f64(x_attn), 2, "e4m3")
    w1 = f64(cw1)
    a = xq @ mxq(w1[:D], 0, "e4m3")
    e = xq @ mxq(w1[D:], 0, "e4m3")
    i, j = np.tril_indices(L)
    h2 = gelu(a[:, i] + e[:, j] + f64(cb1))
    y = (mxq(h2, 2, "e4m3") @ mxq(f64(cw2), 0, "e4m3")) + f64(cb2)
    rel = layer_norm(y, f64(cln_g), f64(cln_b))
    full = np.zeros((B, L, L, D))
    full[:, i, j] = rel
    return full.mean(axis=2)

@@ -1,0 +1,411 @@
+from contextlib import ExitStack
+
+import concourse.mybir as mybir
+from concourse.masks import make_identity
+
+F32 = mybir.dt.float32
+BF16 = mybir.dt.bfloat16
+U32 = mybir.dt.uint32
+U8 = mybir.dt.uint8
+I32 = mybir.dt.int32
+FP8X4 = mybir.dt.float8_e4m3fn_x4
+ALU = mybir.AluOpType
+ACT = mybir.ActivationFunctionType
+
+P = 128
+B, L, D, C = 8, 32, 1024, 512
+EPS = 1e-5
+FLOPS = 2 * (B * L) * (2 * D) * C + 2 * (B * L * (L + 1) // 2) * C * D
+
+GROUPS = [1] + [2] * 16
+Z_ON_SCALAR = (3, 8, 13, 19, 24, 29)
+LAG_ADD, LAG_GELU, LAG_QUANT, LAG_Z, LAG_SUM = 6, 4, 2, 4, 5
+
+
+def tile_parts():
+    tiles = [(0, [(0, 16, 0)]), (16, [(0, 16, 0)])]
+    for w in range(15, 0, -1):
+        tiles.append((w, [(0, 16 - w, 16 + w), (16 - w, w, 16 - w)]))
+    for n in range(1, 17):
+        tiles.append((0, [(0, 16, n)]))
+    return tiles
+
+
+N_PHASE1 = 17
+
+
+def tile_causalexpert_pa_t_kernel(tc, x_attn, cw1, cb1, cw2, cb2, cln_g, cln_b, out):
+    nc = tc.nc
+    tiles = tile_parts()
+    n_tiles = len(tiles)
+    assert n_tiles == 33 and sum(GROUPS) == n_tiles
+    groups = []
+    first_of = {}
+    last_of = {}
+    group_of = {}
+    t0 = 0
+    for n in GROUPS:
+        first_of[t0] = len(groups)
+        last_of[t0 + n - 1] = len(groups)
+        for t in range(t0, t0 + n):
+            group_of[t] = len(groups)
+        groups.append((t0, n))
+        t0 += n
+    gmax = max(GROUPS)
+
+    with ExitStack() as ctx:
+        const = ctx.enter_context(tc.tile_pool(name="const", bufs=1))
+        hp_pool = ctx.enter_context(tc.tile_pool(name="hp", bufs=4))
+        h2_pool = ctx.enter_context(tc.tile_pool(name="h2", bufs=3))
+        hq_pool = ctx.enter_context(tc.tile_pool(name="hq", bufs=4))
+        y_pool = ctx.enter_context(tc.tile_pool(name="y", bufs=8))
+        z_pool = ctx.enter_context(tc.tile_pool(name="z", bufs=4))
+        junk_pool = ctx.enter_context(tc.tile_pool(name="junk", bufs=2))
+        psum = ctx.enter_context(tc.psum_pool(name="psum", bufs=1))
+        ctx.enter_context(tc.manual_schedule())
+
+        x_sb = const.tile([P, 2048], BF16, name="x_sb")
+        nc.sync.dma_start(
+            out=x_sb[:].rearrange("p (h d) -> p h d", h=2),
+            in_=x_attn.flatten_outer_dims().rearrange("(h p) d -> p h d", p=P),
+        )
+        raw1 = const.tile([P, 8, 1024], BF16, name="raw1")
+        w1_view = cw1.rearrange("(s q e) c -> q s (e c)", s=8, q=P, e=2)
+        for unit in range(4):
+            nc.sync.dma_start(out=raw1[:, 2 * unit : 2 * unit + 2, :], in_=w1_view[:, 2 * unit : 2 * unit + 2, :])
+        raw2 = const.tile([P, 4, 1024], BF16, name="raw2")
+        w2_view = cw2.rearrange("(t p) n -> p t n", p=P)
+        for hf in range(2):
+            nc.sync.dma_start(out=raw2[:, :, 512 * hf : 512 * hf + 512], in_=w2_view[:, :, 512 * hf : 512 * hf + 512])
+        b_bc = const.tile([P, 1024], BF16, name="b_bc")
+        nc.sync.dma_start(out=b_bc[:], in_=cln_b.partition_broadcast(P))
+
+        sm = const.tile([P, P], BF16, name="sm")
+        nc.vector.memset(sm[:], 0.0)
+        cbrow = const.tile([P, 1024], BF16, name="cbrow")
+        nc.vector.memset(cbrow[:], 0.0)
+        nc.scalar.dma_start(out=sm[0:8, :], in_=cln_g.rearrange("(c p) -> c p", p=P))
+        nc.scalar.dma_start(out=sm[8:12, :], in_=cb1.rearrange("(t p) -> t p", p=P))
+        nc.scalar.dma_start(out=cbrow[0:1, :], in_=cb2.rearrange("(o n) -> o n", o=1))
+
+        pidx = const.tile([P, 1], I32, name="pidx")
+        nc.gpsimd.iota(pidx[:], pattern=[[0, 1]], base=0, channel_multiplier=1)
+        ident_b = const.tile([P, P], BF16, name="ident_b")
+        make_identity(nc, ident_b[:])
+        ident_f = const.tile([P, P], F32, name="ident_f")
+        make_identity(nc, ident_f[:])
+        ones_b = const.tile([P, P], BF16, name="ones_b")
+        nc.vector.memset(ones_b[:], 1.0)
+        mhalf = const.tile([P, 4], F32, name="mhalf")
+        nc.vector.memset(mhalf[:], -0.5)
+        kidx = const.tile([P, 1], I32, name="kidx")
+        nc.vector.tensor_single_scalar(out=kidx[:], in_=pidx[:], scalar=15, op=ALU.bitwise_and)
+        kf = const.tile([P, 1], F32, name="kf")
+        nc.vector.tensor_copy(out=kf[:], in_=kidx[:])
+        cnt = {}
+        for a, sign, base in (("H", 1.0, 17.0), ("L", -1.0, 16.0)):
+            cnt[a] = const.tile([P, 1], F32, name="cnt" + a)
+            nc.vector.tensor_scalar(out=cnt[a][:], in0=kf[:], scalar1=sign / 32.0, scalar2=base / 32.0, op0=ALU.mult, op1=ALU.add)
+
+        sm_ps = psum.tile([P, P], BF16, name="sm_ps", tag="y2")
+        nc.tensor.transpose(sm_ps[:], sm[:], ident_b[:])
+        smT = const.tile([P, 12], F32, name="smT")
+        nc.vector.tensor_copy(out=smT[:], in_=sm_ps[:, 0:12])
+
+        cb2_bc = const.tile([P, 1024], F32, name="cb2_bc")
+        for hf in range(2):
+            cb_ps = psum.tile([P, 512], F32, name="cb_ps%d" % hf, tag="p%s1" % "ab"[hf])
+            nc.tensor.matmul(cb_ps[:], lhsT=ones_b[:], rhs=cbrow[:, 512 * hf : 512 * hf + 512], start=True, stop=True)
+            nc.scalar.copy(out=cb2_bc[:, 512 * hf : 512 * hf + 512], in_=cb_ps[:])
+
+        xw = x_sb[:].bitcast(F32)
+        xg = const.tile([P, 2048], BF16, name="xg", align_bytes=64)
+        xgw = xg[:].bitcast(F32)
+        for g in range(2):
+            xt = psum.tile([P, 2, 2, P], F32, name="xt%d" % g, tag="y%d" % g)
+            for h in range(2):
+                for u in range(2):
+                    col = 512 * h + 256 * g + 128 * u
+                    nc.tensor.transpose(xt[:, h, u, :], xw[:, col : col + 128], ident_f[:])
+            dst = xgw[:, 512 * g : 512 * g + 512].rearrange("p (h r u) -> p h r u", h=2, u=2)
+            src = xt[:].rearrange("p h u r -> p h r u")
+            if g == 0:
+                nc.vector.tensor_copy(out=dst, in_=src)
+            else:
+                nc.scalar.copy(out=dst, in_=src)
+        xq = const.tile([P, 512], U32, name="xq", align_bytes=64)
+        xs = const.tile([P, 512], U8, name="xs", align_bytes=64)
+
+        def regroup(engine, dst, src):
+            d = dst.rearrange("p (c i) t -> p c t i", i=4)
+            s = src.rearrange("p t (c i) -> p c t i", i=4)
+            if engine == "v":
+                nc.vector.tensor_copy(out=d, in_=s)
+            else:
+                nc.scalar.copy(out=d, in_=s)
+
+        w1q = const.tile([P, 2048], U32, name="w1q", align_bytes=64)
+        w1s = const.tile([P, 2048], U8, name="w1s", align_bytes=64)
+        w1g = [const.tile([P, 512, 4], BF16, name="w1g%d" % unit, align_bytes=64) for unit in range(4)]
+        w2q = const.tile([P, 1024], U32, name="w2q", align_bytes=64)
+        w2s = const.tile([P, 1024], U8, name="w2s", align_bytes=64)
+        w2g = [const.tile([P, 512, 4], BF16, name="w2g%d" % hf, align_bytes=64) for hf in range(2)]
+
+        def regroup1(engine, unit):
+            regroup(engine, w1g[unit][:], raw1[:, 2 * unit : 2 * unit + 2, :].rearrange("p u (e c) -> p (u e) c", e=2))
+
+        def quant1(unit):
+            nc.vector.quantize_mx(
+                out=w1q[:, 512 * unit : 512 * unit + 512].bitcast(FP8X4),
+                scales=w1s[:, 512 * unit : 512 * unit + 512],
+                in_=w1g[unit][:].rearrange("p c t -> p (c t)"),
+            )
+
+        def quant2(hf):
+            nc.vector.quantize_mx(
+                out=w2q[:, 512 * hf : 512 * hf + 512].bitcast(FP8X4),
+                scales=w2s[:, 512 * hf : 512 * hf + 512],
+                in_=w2g[hf][:].rearrange("p c t -> p (c t)"),
+            )
+
+        a_pos = const.tile([P, B, 32, 4], F32, name="a_pos")
+        a_low = const.tile([P, B, 16, 4], F32, name="a_low")
+        eT = const.tile([P, 256, 4], F32, name="eT")
+        ps1 = {}
+
+        def first_mm(half):
+            for h in range(2):
+                ps1[(half, h)] = psum.tile([P, 4, P], F32, name="ps1_%d%d" % (half, h), tag=(("y2", "y3"), ("pa0", "pb0"))[half][h])
+                for t2 in range(4):
+                    for g in range(2):
+                        wc = 512 * (2 * half + g) + 128 * t2
+                        xc = 256 * g + 128 * h
+                        nc.tensor.matmul_mx(
+                            out=ps1[(half, h)][:, t2, :],
+                            lhsT=w1q[:, wc : wc + 128].bitcast(FP8X4),
+                            lhsT_scale=w1s[:, wc : wc + 128],
+                            rhs=xq[:, xc : xc + 128].bitcast(FP8X4),
+                            rhs_scale=xs[:, xc : xc + 128],
+                            start=(g == 0),
+                            stop=(g == 1),
+                        )
+
+        regroup1("v", 0)
+        regroup1("s", 1)
+        nc.vector.quantize_mx(out=xq[:].bitcast(FP8X4), scales=xs[:], in_=xg[:])
+        regroup1("v", 2)
+        quant1(0)
+        quant1(1)
+        first_mm(0)
+        regroup1("v", 3)
+        quant1(2)
+        quant1(3)
+        first_mm(1)
+        regroup("s", w2g[0][:], raw2[:, :, 0:512])
+        bias = smT[:, 8:12].unsqueeze(1).unsqueeze(1).to_broadcast([P, 4, 16, 4])
+        for h in range(2):
+            src4 = ps1[(0, h)][:].rearrange("p t (b i) -> p b i t", b=4)
+            nc.vector.tensor_tensor(out=a_pos[:, 4 * h : 4 * h + 4, 0:16, :], in0=src4[:, :, 16:32, :], in1=bias, op=ALU.add)
+        for h in range(2):
+            src4 = ps1[(0, h)][:].rearrange("p t (b i) -> p b i t", b=4)
+            nc.vector.tensor_tensor(out=a_low[:, 4 * h : 4 * h + 4, :, :], in0=src4[:, :, 0:16, :], in1=bias, op=ALU.add)
+        for h in range(2):
+            nc.scalar.copy(out=eT[:, 128 * h : 128 * h + 128, :], in_=ps1[(1, h)][:].rearrange("p t r -> p r t"))
+        for k in range(16):
+            nc.scalar.copy(out=a_pos[:, :, 16 + k, :], in_=a_low[:, :, 15 - k, :])
+        regroup("v", w2g[1][:], raw2[:, :, 512:1024])
+        quant2(0)
+        quant2(1)
+        e4 = eT[:].rearrange("p (b i) t -> p b i t", b=B)
+
+        ssum = const.tile([P, 2 * n_tiles], F32, name="ssum")
+        nm = const.tile([P, n_tiles], F32, name="nm")
+        ssq = const.tile([P, n_tiles], F32, name="ssq")
+        tv = const.tile([P, n_tiles], F32, name="tv")
+        wv = const.tile([P, n_tiles], F32, name="wv")
+        nmw = const.tile([P, n_tiles], F32, name="nmw")
+
+        acc = {}
+        hp_t = {}
+        h2_t = {}
+        hq_t = {}
+        yps_t = {}
+        y_t = {}
+        z_t = {}
+        ident3 = ident_f[:].rearrange("p (b s) -> p b s", b=B)
+
+        def stage_add(g):
+            t0, n = groups[g]
+            hp_t[g] = hp_pool.tile([P, 512 * gmax], F32, name="hp")
+            for ti in range(n):
+                view = hp_t[g][:, 512 * ti : 512 * ti + 512].rearrange("p (b s t) -> p b s t", b=B, t=4)
+                w, parts = tiles[t0 + ti]
+                for s0, ns, j in parts:
+                    nc.gpsimd.tensor_tensor(
+                        out=view[:, :, s0 : s0 + ns, :],
+                        in0=a_pos[:, :, w + s0 : w + s0 + ns, :],
+                        in1=e4[:, :, j : j + 1, :].to_broadcast([P, B, ns, 4]),
+                        op=ALU.add,
+                    )
+
+        def stage_gelu(g):
+            n = groups[g][1]
+            h2_t[g] = h2_pool.tile([P, 512 * gmax], BF16, name="h2", align_bytes=64)
+            nc.scalar.activation(out=h2_t[g][:, 0 : 512 * n], in_=hp_t[g][:, 0 : 512 * n], func=ACT.Gelu)
+
+        def stage_quant(g):
+            n = groups[g][1]
+            hq = hq_pool.tile([P, 128 * gmax], U32, name="hq", align_bytes=64)
+            hs = hq_pool.tile([P, 128 * gmax], U8, name="hs", align_bytes=64)
+            hq_t[g] = (hq, hs)
+            nc.vector.quantize_mx(out=hq[:, 0 : 128 * n].bitcast(FP8X4), scales=hs[:, 0 : 128 * n], in_=h2_t[g][:, 0 : 512 * n])
+
+        def stage_mm(t):
+            g = group_of[t]
+            ti = t - groups[g][0]
+            hq, hs = hq_t[g]
+            for hf in range(2):
+                yps_t[(t, hf)] = psum.tile([P, 512], F32, name="yps", tag="y%d" % (2 * (t % 2) + hf))
+                nc.tensor.matmul_mx(
+                    out=yps_t[(t, hf)][:],
+                    lhsT=hq[:, 128 * ti : 128 * ti + 128].bitcast(FP8X4),
+                    lhsT_scale=hs[:, 128 * ti : 128 * ti + 128],
+                    rhs=w2q[:, 512 * hf : 512 * hf + 512].bitcast(FP8X4),
+                    rhs_scale=w2s[:, 512 * hf : 512 * hf + 512],
+                    start=True,
+                    stop=True,
+                )
+
+        def stage_bias(t):
+            y_t[t] = y_pool.tile([P, 1024], F32, name="y")
+            for hf in range(2):
+                nc.vector.scalar_tensor_tensor(
+                    out=y_t[t][:, 512 * hf : 512 * hf + 512],
+                    in0=yps_t[(t, hf)][:],
+                    scalar=1.0,
+                    in1=cb2_bc[:, 512 * hf : 512 * hf + 512],
+                    op0=ALU.mult,
+                    op1=ALU.add,
+                    accum_out=ssum[:, 2 * t + hf : 2 * t + hf + 1],
+                )
+            nc.vector.tensor_scalar(
+                out=nm[:, t : t + 1],
+                in0=ssum[:, 2 * t : 2 * t + 1],
+                scalar1=ssum[:, 2 * t + 1 : 2 * t + 2],
+                scalar2=-1.0 / D,
+                op0=ALU.add,
+                op1=ALU.mult,
+            )
+
+        def stage_square(t):
+            junk = junk_pool.tile([P, 1024], BF16, name="junk")
+            nc.scalar.activation(out=junk[:], in_=y_t[t][:], func=ACT.Square, bias=nm[:, t : t + 1], scale=1.0, accum_out=ssq[:, t : t + 1])
+
+        def stage_weight(g):
+            t0, n = groups[g]
+            sl = slice(t0, t0 + n)
+            nc.gpsimd.tensor_scalar(out=tv[:, sl], in0=ssq[:, sl], scalar1=1.0, scalar2=D * EPS, op0=ALU.mult, op1=ALU.add)
+            nc.gpsimd.tensor_tensor(out=wv[:, sl], in0=tv[:, sl], in1=mhalf[:, 0:n], op=ALU.pow)
+            nc.gpsimd.tensor_tensor(out=nmw[:, sl], in0=nm[:, sl], in1=wv[:, sl], op=ALU.mult)
+
+        def stage_z(t):
+            z_t[t] = z_pool.tile([P, 1024], F32, name="z")
+            if t in Z_ON_SCALAR:
+                nc.scalar.activation(out=z_t[t][:], in_=y_t[t][:], func=ACT.Identity, bias=nmw[:, t : t + 1], scale=wv[:, t : t + 1])
+            else:
+                nc.vector.tensor_scalar(
+                    out=z_t[t][:], in0=y_t[t][:], scalar1=wv[:, t : t + 1], scalar2=nmw[:, t : t + 1], op0=ALU.mult, op1=ALU.add
+                )
+
+        def stage_sum(t):
+            w = tiles[t][0]
+            for c in range(8):
+                if t < N_PHASE1:
+                    key = (1, c // 2)
+                    if key not in acc:
+                        acc[key] = psum.tile([P, 2, B, 32], F32, name="acc1_%d" % (c // 2), tag="p%s%d" % ("ab"[c // 4], (c // 2) % 2))
+                    dst = acc[key][:, c % 2, :, w : w + 16]
+                    first = t == 0 and c % 2 == 0
+                    last = t == N_PHASE1 - 1 and c % 2 == 1
+                else:
+                    key = (2, c // 4)
+                    if key not in acc:
+                        acc[key] = psum.tile([P, 4, B, 16], F32, name="acc2_%d" % (c // 4), tag="pa%d" % (c // 4))
+                    dst = acc[key][:, c % 4, :, :]
+                    first = t == N_PHASE1 and c % 4 == 0
+                    last = t == n_tiles - 1 and c % 4 == 3
+                nc.tensor.matmul(dst, lhsT=z_t[t][:, 128 * c : 128 * c + 128], rhs=ident3, is_transpose=True, start=first, stop=last)
+
+        oT = {}
+        for a in "HL":
+            oT[a] = const.tile([P, 8, B, 16], F32, name="oT" + a)
+
+        def stage_mid():
+            for bank in range(2):
+                gain = smT[:, 2 * bank : 2 * bank + 2].unsqueeze(2).unsqueeze(3).to_broadcast([P, 2, B, 16])
+                for a, p0 in (("H", 0), ("L", 16)):
+                    nc.vector.tensor_tensor(
+                        out=oT[a][:, 2 * bank : 2 * bank + 2, :, :], in0=acc[(1, bank)][:, :, :, p0 : p0 + 16], in1=gain, op=ALU.mult
+                    )
+            for c in range(4, 8):
+                for a, p0 in (("H", 0), ("L", 16)):
+                    nc.scalar.activation(
+                        out=oT[a][:, c, :, :], in_=acc[(1, c // 2)][:, c % 2, :, p0 : p0 + 16], func=ACT.Copy, scale=smT[:, c : c + 1]
+                    )
+
+        def stage_last():
+            for c in range(8):
+                nc.vector.scalar_tensor_tensor(
+                    out=oT["H"][:, c, :, :].rearrange("p b s -> p (b s)"),
+                    in0=acc[(2, c // 4)][:, c % 4, :, :].rearrange("p b s -> p (b s)"),
+                    scalar=smT[:, c : c + 1],
+                    in1=oT["H"][:, c, :, :].rearrange("p b s -> p (b s)"),
+                    op0=ALU.mult,
+                    op1=ALU.add,
+                )
+
+        def stage_out(a):
+            osb = const.tile([P, 1024], F32, name="osb" + a)
+            for hb in range(2):
+                back = psum.tile([P, 512], F32, name="back%s%d" % (a, hb), tag="pb%d" % hb)
+                for c in range(4):
+                    nc.tensor.transpose(back[:, 128 * c : 128 * c + 128], oT[a][:, 4 * hb + c, :, :].rearrange("p b s -> p (b s)"), ident_f[:])
+                nc.vector.scalar_tensor_tensor(
+                    out=osb[:, 512 * hb : 512 * hb + 512],
+                    in0=b_bc[:, 512 * hb : 512 * hb + 512],
+                    scalar=cnt[a][:, 0:1],
+                    in1=back[:],
+                    op0=ALU.mult,
+                    op1=ALU.add,
+                )
+            if a == "H":
+                for b in range(B):
+                    nc.sync.dma_start(out=out[b, 16:32, :], in_=osb[16 * b : 16 * b + 16, :])
+            else:
+                for k in range(16):
+                    nc.sync.dma_start(out=out[:, 15 - k, :], in_=osb[k : P : 16, :])
+
+        for step in range(-LAG_ADD, n_tiles + LAG_SUM):
+            if step + LAG_ADD in first_of:
+                stage_add(first_of[step + LAG_ADD])
+            if step + LAG_GELU in first_of:
+                stage_gelu(first_of[step + LAG_GELU])
+            if step + LAG_QUANT in first_of:
+                stage_quant(first_of[step + LAG_QUANT])
+            if 0 <= step + 1 < n_tiles:
+                stage_mm(step + 1)
+            if 0 <= step < n_tiles:
+                stage_bias(step)
+                stage_square(step)
+            if step in last_of:
+                stage_weight(last_of[step])
+            if 0 <= step - LAG_Z < n_tiles:
+                stage_z(step - LAG_Z)
+            if 0 <= step - LAG_SUM < n_tiles:
+                stage_sum(step - LAG_SUM)
+            if step - LAG_SUM == N_PHASE1 - 1:
+                stage_mid()
+            if step - LAG_SUM == N_PHASE1 + 1:
+                stage_out("L")
+        stage_last()
+        stage_out("H")

@@ -19,7 +19,8 @@ FLOPS = 2 * (B * L) * (2 * D) * C + 2 * (B * L * (L + 1) // 2) * C * D
 
 GROUPS = [1] + [2] * 16
 Z_ON_SCALAR = (3, 8, 13, 19, 24, 29)
-LAG_ADD, LAG_GELU, LAG_QUANT, LAG_Z, LAG_SUM = 6, 4, 2, 4, 5
+LAG_ADD, LAG_GELU, LAG_QUANT, LAG_Z, LAG_SUM = 6, 4, 2, 4, 7
+DUP = 1
 
 
 def tile_parts():
@@ -59,7 +60,7 @@ def tile_causalexpert_pa_t_kernel(tc, x_attn, cw1, cb1, cw2, cb2, cln_g, cln_b, 
         h2_pool = ctx.enter_context(tc.tile_pool(name="h2", bufs=3))
         hq_pool = ctx.enter_context(tc.tile_pool(name="hq", bufs=4))
         y_pool = ctx.enter_context(tc.tile_pool(name="y", bufs=8))
-        z_pool = ctx.enter_context(tc.tile_pool(name="z", bufs=4))
+        z_pool = ctx.enter_context(tc.tile_pool(name="z", bufs=6))
         junk_pool = ctx.enter_context(tc.tile_pool(name="junk", bufs=2))
         psum = ctx.enter_context(tc.psum_pool(name="psum", bufs=1))
         ctx.enter_context(tc.manual_schedule())
@@ -266,15 +267,16 @@ def tile_causalexpert_pa_t_kernel(tc, x_attn, cw1, cb1, cw2, cb2, cln_g, cln_b, 
             hq, hs = hq_t[g]
             for hf in range(2):
                 yps_t[(t, hf)] = psum.tile([P, 512], F32, name="yps", tag="y%d" % (2 * (t % 2) + hf))
-                nc.tensor.matmul_mx(
-                    out=yps_t[(t, hf)][:],
-                    lhsT=hq[:, 128 * ti : 128 * ti + 128].bitcast(FP8X4),
-                    lhsT_scale=hs[:, 128 * ti : 128 * ti + 128],
-                    rhs=w2q[:, 512 * hf : 512 * hf + 512].bitcast(FP8X4),
-                    rhs_scale=w2s[:, 512 * hf : 512 * hf + 512],
-                    start=True,
-                    stop=True,
-                )
+                for rep in range(1 + (DUP if hf == 0 else 0)):
+                    nc.tensor.matmul_mx(
+                        out=yps_t[(t, hf)][:],
+                        lhsT=hq[:, 128 * ti : 128 * ti + 128].bitcast(FP8X4),
+                        lhsT_scale=hs[:, 128 * ti : 128 * ti + 128],
+                        rhs=w2q[:, 512 * hf : 512 * hf + 512].bitcast(FP8X4),
+                        rhs_scale=w2s[:, 512 * hf : 512 * hf + 512],
+                        start=True,
+                        stop=True,
+                    )
 
         def stage_bias(t):
             y_t[t] = y_pool.tile([P, 1024], F32, name="y")
@@ -306,15 +308,15 @@ def tile_causalexpert_pa_t_kernel(tc, x_attn, cw1, cb1, cw2, cb2, cln_g, cln_b, 
             sl = slice(t0, t0 + n)
             nc.gpsimd.tensor_scalar(out=tv[:, sl], in0=ssq[:, sl], scalar1=1.0, scalar2=D * EPS, op0=ALU.mult, op1=ALU.add)
             nc.gpsimd.tensor_tensor(out=wv[:, sl], in0=tv[:, sl], in1=mhalf[:, 0:n], op=ALU.pow)
-            nc.gpsimd.tensor_tensor(out=nmw[:, sl], in0=nm[:, sl], in1=wv[:, sl], op=ALU.mult)
 
         def stage_z(t):
             z_t[t] = z_pool.tile([P, 1024], F32, name="z")
             if t in Z_ON_SCALAR:
+                nc.vector.tensor_tensor(out=nmw[:, t : t + 1], in0=nm[:, t : t + 1], in1=wv[:, t : t + 1], op=ALU.mult)
                 nc.scalar.activation(out=z_t[t][:], in_=y_t[t][:], func=ACT.Identity, bias=nmw[:, t : t + 1], scale=wv[:, t : t + 1])
             else:
                 nc.vector.tensor_scalar(
-                    out=z_t[t][:], in0=y_t[t][:], scalar1=wv[:, t : t + 1], scalar2=nmw[:, t : t + 1], op0=ALU.mult, op1=ALU.add
+                    out=z_t[t][:], in0=y_t[t][:], scalar1=nm[:, t : t + 1], scalar2=wv[:, t : t + 1], op0=ALU.add, op1=ALU.mult
                 )
 
         def stage_sum(t):
@@ -390,13 +392,13 @@ def tile_causalexpert_pa_t_kernel(tc, x_attn, cw1, cb1, cw2, cb2, cln_g, cln_b, 
                 stage_add(first_of[step + LAG_ADD])
             if step + LAG_GELU in first_of:
                 stage_gelu(first_of[step + LAG_GELU])
-            if step + LAG_QUANT in first_of:
-                stage_quant(first_of[step + LAG_QUANT])
             if 0 <= step + 1 < n_tiles:
                 stage_mm(step + 1)
             if 0 <= step < n_tiles:
                 stage_bias(step)
                 stage_square(step)
+            if step + LAG_QUANT in first_of:
+                stage_quant(first_of[step + LAG_QUANT])
             if step in last_of:
                 stage_weight(last_of[step])
             if 0 <= step - LAG_Z < n_tiles:

@@ -18,9 +18,14 @@ EPS = 1e-5
 FLOPS = 2 * (B * L) * (2 * D) * C + 2 * (B * L * (L + 1) // 2) * C * D
 
 GROUPS = [1] + [2] * 16
-Z_ON_SCALAR = (3, 8, 13, 19, 24, 29)
 LAG_ADD, LAG_GELU, LAG_QUANT, LAG_Z, LAG_SUM = 6, 4, 2, 4, 7
-DUP = 1
+DUP = 0
+
+
+def z_engine(t):
+    if t >= 30:
+        return "v"
+    return "s" if t % 3 == 1 else "g"
 
 
 def tile_parts():
@@ -78,8 +83,6 @@ def tile_causalexpert_pa_t_kernel(tc, x_attn, cw1, cb1, cw2, cb2, cln_g, cln_b, 
         w2_view = cw2.rearrange("(t p) n -> p t n", p=P)
         for hf in range(2):
             nc.sync.dma_start(out=raw2[:, :, 512 * hf : 512 * hf + 512], in_=w2_view[:, :, 512 * hf : 512 * hf + 512])
-        b_bc = const.tile([P, 1024], BF16, name="b_bc")
-        nc.sync.dma_start(out=b_bc[:], in_=cln_b.partition_broadcast(P))
 
         sm = const.tile([P, P], BF16, name="sm")
         nc.vector.memset(sm[:], 0.0)
@@ -87,10 +90,13 @@ def tile_causalexpert_pa_t_kernel(tc, x_attn, cw1, cb1, cw2, cb2, cln_g, cln_b, 
         nc.vector.memset(cbrow[:], 0.0)
         nc.scalar.dma_start(out=sm[0:8, :], in_=cln_g.rearrange("(c p) -> c p", p=P))
         nc.scalar.dma_start(out=sm[8:12, :], in_=cb1.rearrange("(t p) -> t p", p=P))
+        nc.scalar.dma_start(out=sm[12:20, :], in_=cln_b.rearrange("(c p) -> c p", p=P))
         nc.scalar.dma_start(out=cbrow[0:1, :], in_=cb2.rearrange("(o n) -> o n", o=1))
 
-        pidx = const.tile([P, 1], I32, name="pidx")
-        nc.gpsimd.iota(pidx[:], pattern=[[0, 1]], base=0, channel_multiplier=1)
+        cnt_i = {}
+        for a, step_k, base in (("H", 1, 17), ("L", -1, 16)):
+            cnt_i[a] = const.tile([P, P], I32, name="cnt_i" + a)
+            nc.gpsimd.iota(cnt_i[a][:], pattern=[[0, B], [step_k, 16]], base=base, channel_multiplier=0)
         ident_b = const.tile([P, P], BF16, name="ident_b")
         make_identity(nc, ident_b[:])
         ident_f = const.tile([P, P], F32, name="ident_f")
@@ -99,19 +105,22 @@ def tile_causalexpert_pa_t_kernel(tc, x_attn, cw1, cb1, cw2, cb2, cln_g, cln_b, 
         nc.vector.memset(ones_b[:], 1.0)
         mhalf = const.tile([P, 4], F32, name="mhalf")
         nc.vector.memset(mhalf[:], -0.5)
-        kidx = const.tile([P, 1], I32, name="kidx")
-        nc.vector.tensor_single_scalar(out=kidx[:], in_=pidx[:], scalar=15, op=ALU.bitwise_and)
-        kf = const.tile([P, 1], F32, name="kf")
-        nc.vector.tensor_copy(out=kf[:], in_=kidx[:])
-        cnt = {}
-        for a, sign, base in (("H", 1.0, 17.0), ("L", -1.0, 16.0)):
-            cnt[a] = const.tile([P, 1], F32, name="cnt" + a)
-            nc.vector.tensor_scalar(out=cnt[a][:], in0=kf[:], scalar1=sign / 32.0, scalar2=base / 32.0, op0=ALU.mult, op1=ALU.add)
+        cnt_f = {}
+        for a in "HL":
+            cnt_f[a] = const.tile([P, P], F32, name="cnt_f" + a)
+            nc.vector.tensor_copy(out=cnt_f[a][:], in_=cnt_i[a][:])
 
         sm_ps = psum.tile([P, P], BF16, name="sm_ps", tag="y2")
         nc.tensor.transpose(sm_ps[:], sm[:], ident_b[:])
-        smT = const.tile([P, 12], F32, name="smT")
-        nc.vector.tensor_copy(out=smT[:], in_=sm_ps[:, 0:12])
+        smT = const.tile([P, 20], F32, name="smT")
+        nc.vector.tensor_copy(out=smT[:], in_=sm_ps[:, 0:20])
+        bcT = {}
+        for a in "LH":
+            bcT[a] = const.tile([P, 8, P], F32, name="bcT" + a)
+            for c in range(8):
+                nc.gpsimd.tensor_scalar(
+                    out=bcT[a][:, c, :], in0=cnt_f[a][:], scalar1=smT[:, 12 + c : 13 + c], scalar2=1.0 / 32.0, op0=ALU.mult, op1=ALU.mult
+                )
 
         cb2_bc = const.tile([P, 1024], F32, name="cb2_bc")
         for hf in range(2):
@@ -242,7 +251,7 @@ def tile_causalexpert_pa_t_kernel(tc, x_attn, cw1, cb1, cw2, cb2, cln_g, cln_b, 
                 view = hp_t[g][:, 512 * ti : 512 * ti + 512].rearrange("p (b s t) -> p b s t", b=B, t=4)
                 w, parts = tiles[t0 + ti]
                 for s0, ns, j in parts:
-                    nc.gpsimd.tensor_tensor(
+                    nc.vector.tensor_tensor(
                         out=view[:, :, s0 : s0 + ns, :],
                         in0=a_pos[:, :, w + s0 : w + s0 + ns, :],
                         in1=e4[:, :, j : j + 1, :].to_broadcast([P, B, ns, 4]),
@@ -308,12 +317,18 @@ def tile_causalexpert_pa_t_kernel(tc, x_attn, cw1, cb1, cw2, cb2, cln_g, cln_b, 
             sl = slice(t0, t0 + n)
             nc.gpsimd.tensor_scalar(out=tv[:, sl], in0=ssq[:, sl], scalar1=1.0, scalar2=D * EPS, op0=ALU.mult, op1=ALU.add)
             nc.gpsimd.tensor_tensor(out=wv[:, sl], in0=tv[:, sl], in1=mhalf[:, 0:n], op=ALU.pow)
+            if any(z_engine(t) == "s" for t in range(t0, t0 + n)):
+                nc.gpsimd.tensor_tensor(out=nmw[:, sl], in0=nm[:, sl], in1=wv[:, sl], op=ALU.mult)
 
         def stage_z(t):
             z_t[t] = z_pool.tile([P, 1024], F32, name="z")
-            if t in Z_ON_SCALAR:
-                nc.vector.tensor_tensor(out=nmw[:, t : t + 1], in0=nm[:, t : t + 1], in1=wv[:, t : t + 1], op=ALU.mult)
+            eng = z_engine(t)
+            if eng == "s":
                 nc.scalar.activation(out=z_t[t][:], in_=y_t[t][:], func=ACT.Identity, bias=nmw[:, t : t + 1], scale=wv[:, t : t + 1])
+            elif eng == "g":
+                nc.gpsimd.tensor_scalar(
+                    out=z_t[t][:], in0=y_t[t][:], scalar1=nm[:, t : t + 1], scalar2=wv[:, t : t + 1], op0=ALU.add, op1=ALU.mult
+                )
             else:
                 nc.vector.tensor_scalar(
                     out=z_t[t][:], in0=y_t[t][:], scalar1=nm[:, t : t + 1], scalar2=wv[:, t : t + 1], op0=ALU.add, op1=ALU.mult
@@ -339,53 +354,59 @@ def tile_causalexpert_pa_t_kernel(tc, x_attn, cw1, cb1, cw2, cb2, cln_g, cln_b, 
                 nc.tensor.matmul(dst, lhsT=z_t[t][:, 128 * c : 128 * c + 128], rhs=ident3, is_transpose=True, start=first, stop=last)
 
         oT = {}
-        for a in "HL":
+        for a in ("L", "H1", "H2"):
             oT[a] = const.tile([P, 8, B, 16], F32, name="oT" + a)
+        back = {}
 
         def stage_mid():
             for bank in range(2):
                 gain = smT[:, 2 * bank : 2 * bank + 2].unsqueeze(2).unsqueeze(3).to_broadcast([P, 2, B, 16])
-                for a, p0 in (("H", 0), ("L", 16)):
+                for a, p0 in (("L", 16), ("H1", 0)):
                     nc.vector.tensor_tensor(
                         out=oT[a][:, 2 * bank : 2 * bank + 2, :, :], in0=acc[(1, bank)][:, :, :, p0 : p0 + 16], in1=gain, op=ALU.mult
                     )
-            for c in range(4, 8):
-                for a, p0 in (("H", 0), ("L", 16)):
+            for a, p0 in (("L", 16), ("H1", 0)):
+                for c in range(4, 8):
                     nc.scalar.activation(
                         out=oT[a][:, c, :, :], in_=acc[(1, c // 2)][:, c % 2, :, p0 : p0 + 16], func=ACT.Copy, scale=smT[:, c : c + 1]
                     )
 
-        def stage_last():
-            for c in range(8):
-                nc.vector.scalar_tensor_tensor(
-                    out=oT["H"][:, c, :, :].rearrange("p b s -> p (b s)"),
-                    in0=acc[(2, c // 4)][:, c % 4, :, :].rearrange("p b s -> p (b s)"),
-                    scalar=smT[:, c : c + 1],
-                    in1=oT["H"][:, c, :, :].rearrange("p b s -> p (b s)"),
-                    op0=ALU.mult,
-                    op1=ALU.add,
-                )
-
-        def stage_out(a):
-            osb = const.tile([P, 1024], F32, name="osb" + a)
+        def stage_back(a, sources, opens, closes):
             for hb in range(2):
-                back = psum.tile([P, 512], F32, name="back%s%d" % (a, hb), tag="pb%d" % hb)
-                for c in range(4):
-                    nc.tensor.transpose(back[:, 128 * c : 128 * c + 128], oT[a][:, 4 * hb + c, :, :].rearrange("p b s -> p (b s)"), ident_f[:])
-                nc.vector.scalar_tensor_tensor(
-                    out=osb[:, 512 * hb : 512 * hb + 512],
-                    in0=b_bc[:, 512 * hb : 512 * hb + 512],
-                    scalar=cnt[a][:, 0:1],
-                    in1=back[:],
-                    op0=ALU.mult,
-                    op1=ALU.add,
-                )
+                if opens:
+                    back[(a, hb)] = psum.tile([P, 512], F32, name="back%s%d" % (a, hb), tag="pb%d" % hb)
+                for n_src, src in enumerate(sources):
+                    for c in range(4):
+                        nc.tensor.matmul(
+                            back[(a, hb)][:, 128 * c : 128 * c + 128],
+                            lhsT=src[:, 4 * hb + c, :],
+                            rhs=ident_f[:],
+                            is_transpose=True,
+                            start=(opens and n_src == 0 and c == 0),
+                            stop=(closes and n_src == len(sources) - 1 and c == 3),
+                        )
+
+        def stage_last():
+            gain = smT[:, 0:4].unsqueeze(2).to_broadcast([P, 4, P])
+            nc.vector.tensor_tensor(
+                out=oT["H2"][:, 0:4, :, :].rearrange("p c b s -> p c (b s)"), in0=acc[(2, 0)][:].rearrange("p c b s -> p c (b s)"), in1=gain, op=ALU.mult
+            )
+            for c in range(4, 8):
+                nc.scalar.activation(out=oT["H2"][:, c, :, :], in_=acc[(2, 1)][:, c % 4, :, :], func=ACT.Copy, scale=smT[:, c : c + 1])
+
+        def stage_store(a):
+            osb = const.tile([P, 1024], F32, name="osb" + a)
+            nc.vector.tensor_copy(out=osb[:, 0:512], in_=back[(a, 0)][:])
+            nc.scalar.copy(out=osb[:, 512:1024], in_=back[(a, 1)][:])
             if a == "H":
                 for b in range(B):
                     nc.sync.dma_start(out=out[b, 16:32, :], in_=osb[16 * b : 16 * b + 16, :])
             else:
                 for k in range(16):
                     nc.sync.dma_start(out=out[:, 15 - k, :], in_=osb[k : P : 16, :])
+
+        def flat(tile_ap):
+            return tile_ap.rearrange("p c b s -> p c (b s)")
 
         for step in range(-LAG_ADD, n_tiles + LAG_SUM):
             if step + LAG_ADD in first_of:
@@ -408,6 +429,10 @@ def tile_causalexpert_pa_t_kernel(tc, x_attn, cw1, cb1, cw2, cb2, cln_g, cln_b, 
             if step - LAG_SUM == N_PHASE1 - 1:
                 stage_mid()
             if step - LAG_SUM == N_PHASE1 + 1:
-                stage_out("L")
+                stage_back("L", [bcT["L"][:], flat(oT["L"][:])], True, True)
+                stage_store("L")
+            if step - LAG_SUM == N_PHASE1 + 3:
+                stage_back("H", [bcT["H"][:], flat(oT["H1"][:])], True, False)
         stage_last()
-        stage_out("H")
+        stage_back("H", [flat(oT["H2"][:])], False, True)
+        stage_store("H")

@@ -17,15 +17,23 @@ B, L, D, C = 8, 32, 1024, 512
 EPS = 1e-5
 FLOPS = 2 * (B * L) * (2 * D) * C + 2 * (B * L * (L + 1) // 2) * C * D
 
+N_PHASE1 = 17
+N_TILES = 33
 GROUPS = [1] + [2] * 16
-LAG_ADD, LAG_GELU, LAG_QUANT, LAG_Z, LAG_SUM = 6, 4, 2, 4, 7
-DUP = 0
+LEAD = 3
+T_WIDE = 15
+T_RSQ = 16
+LAG_Z, LAG_SUM = 2, 4
+G_ADDS = (2, 6, 10, 14, 18, 22, 26, 30)
+DUP = 1
 
 
-def z_engine(t):
-    if t >= 30:
-        return "v"
-    return "s" if t % 3 == 1 else "g"
+def z_engines(t):
+    if t == N_TILES - 1:
+        return "va"
+    if t == N_TILES - 2:
+        return "gv"
+    return "g"
 
 
 def tile_parts():
@@ -37,33 +45,24 @@ def tile_parts():
     return tiles
 
 
-N_PHASE1 = 17
-
-
 def tile_causalexpert_pa_t_kernel(tc, x_attn, cw1, cb1, cw2, cb2, cln_g, cln_b, out):
     nc = tc.nc
     tiles = tile_parts()
-    n_tiles = len(tiles)
-    assert n_tiles == 33 and sum(GROUPS) == n_tiles
     groups = []
-    first_of = {}
-    last_of = {}
-    group_of = {}
     t0 = 0
     for n in GROUPS:
-        first_of[t0] = len(groups)
-        last_of[t0 + n - 1] = len(groups)
-        for t in range(t0, t0 + n):
-            group_of[t] = len(groups)
         groups.append((t0, n))
         t0 += n
-    gmax = max(GROUPS)
+    n_groups = len(groups)
+    group_of = {}
+    for g in range(n_groups):
+        for t in range(groups[g][0], groups[g][0] + groups[g][1]):
+            group_of[t] = g
 
     with ExitStack() as ctx:
         const = ctx.enter_context(tc.tile_pool(name="const", bufs=1))
         hp_pool = ctx.enter_context(tc.tile_pool(name="hp", bufs=4))
         h2_pool = ctx.enter_context(tc.tile_pool(name="h2", bufs=3))
-        hq_pool = ctx.enter_context(tc.tile_pool(name="hq", bufs=4))
         y_pool = ctx.enter_context(tc.tile_pool(name="y", bufs=8))
         z_pool = ctx.enter_context(tc.tile_pool(name="z", bufs=6))
         junk_pool = ctx.enter_context(tc.tile_pool(name="junk", bufs=2))
@@ -84,55 +83,42 @@ def tile_causalexpert_pa_t_kernel(tc, x_attn, cw1, cb1, cw2, cb2, cln_g, cln_b, 
         for hf in range(2):
             nc.sync.dma_start(out=raw2[:, :, 512 * hf : 512 * hf + 512], in_=w2_view[:, :, 512 * hf : 512 * hf + 512])
 
-        sm = const.tile([P, P], BF16, name="sm")
-        nc.vector.memset(sm[:], 0.0)
-        cbrow = const.tile([P, 1024], BF16, name="cbrow")
-        nc.vector.memset(cbrow[:], 0.0)
-        nc.scalar.dma_start(out=sm[0:8, :], in_=cln_g.rearrange("(c p) -> c p", p=P))
-        nc.scalar.dma_start(out=sm[8:12, :], in_=cb1.rearrange("(t p) -> t p", p=P))
-        nc.scalar.dma_start(out=sm[12:20, :], in_=cln_b.rearrange("(c p) -> c p", p=P))
-        nc.scalar.dma_start(out=cbrow[0:1, :], in_=cb2.rearrange("(o n) -> o n", o=1))
-
-        cnt_i = {}
-        for a, step_k, base in (("H", 1, 17), ("L", -1, 16)):
-            cnt_i[a] = const.tile([P, P], I32, name="cnt_i" + a)
-            nc.gpsimd.iota(cnt_i[a][:], pattern=[[0, B], [step_k, 16]], base=base, channel_multiplier=0)
-        ident_b = const.tile([P, P], BF16, name="ident_b")
-        make_identity(nc, ident_b[:])
         ident_f = const.tile([P, P], F32, name="ident_f")
         make_identity(nc, ident_f[:])
-        ones_b = const.tile([P, P], BF16, name="ones_b")
-        nc.vector.memset(ones_b[:], 1.0)
+        sm = const.tile([P, P], BF16, name="sm")
+        nc.vector.memset(sm[:], 0.0)
+        rows = const.tile([P, 1024], BF16, name="rows")
+        nc.vector.memset(rows[:], 0.0)
+        nc.scalar.dma_start(out=sm[0:8, :], in_=cln_g.rearrange("(c p) -> c p", p=P))
+        nc.scalar.dma_start(out=sm[8:12, :], in_=cb1.rearrange("(t p) -> t p", p=P))
+        nc.scalar.dma_start(out=rows[0:1, :], in_=cb2.rearrange("(o n) -> o n", o=1))
+        nc.scalar.dma_start(out=rows[32:33, :], in_=cln_b.rearrange("(o n) -> o n", o=1))
+        warm = const.tile([P, 2], F32, name="warm")
+        nc.vector.memset(warm[:], 0.0)
+        warm_o = const.tile([P, 2], BF16, name="warm_o")
+        nc.scalar.activation(out=warm_o[:], in_=warm[:], func=ACT.Gelu)
+        ident_b = const.tile([P, P], BF16, name="ident_b")
+        nc.vector.tensor_copy(out=ident_b[:], in_=ident_f[:])
+        pick0 = const.tile([P, P], BF16, name="pick0")
+        nc.vector.memset(pick0[:], 0.0)
+        nc.vector.memset(pick0[0:1, :], 1.0)
         mhalf = const.tile([P, 4], F32, name="mhalf")
         nc.vector.memset(mhalf[:], -0.5)
-        cnt_f = {}
-        for a in "HL":
-            cnt_f[a] = const.tile([P, P], F32, name="cnt_f" + a)
-            nc.vector.tensor_copy(out=cnt_f[a][:], in_=cnt_i[a][:])
-
-        sm_ps = psum.tile([P, P], BF16, name="sm_ps", tag="y2")
-        nc.tensor.transpose(sm_ps[:], sm[:], ident_b[:])
-        smT = const.tile([P, 20], F32, name="smT")
-        nc.vector.tensor_copy(out=smT[:], in_=sm_ps[:, 0:20])
-        bcT = {}
-        for a in "LH":
-            bcT[a] = const.tile([P, 8, P], F32, name="bcT" + a)
-            for c in range(8):
-                nc.gpsimd.tensor_scalar(
-                    out=bcT[a][:, c, :], in0=cnt_f[a][:], scalar1=smT[:, 12 + c : 13 + c], scalar2=1.0 / 32.0, op0=ALU.mult, op1=ALU.mult
-                )
-
-        cb2_bc = const.tile([P, 1024], F32, name="cb2_bc")
-        for hf in range(2):
-            cb_ps = psum.tile([P, 512], F32, name="cb_ps%d" % hf, tag="p%s1" % "ab"[hf])
-            nc.tensor.matmul(cb_ps[:], lhsT=ones_b[:], rhs=cbrow[:, 512 * hf : 512 * hf + 512], start=True, stop=True)
-            nc.scalar.copy(out=cb2_bc[:, 512 * hf : 512 * hf + 512], in_=cb_ps[:])
+        deps = const.tile([P, 1], F32, name="deps")
+        nc.vector.tensor_scalar(out=deps[:], in0=warm[:, 0:1], scalar1=1.0, scalar2=D * EPS, op0=ALU.mult, op1=ALU.add)
+        cnt = {}
+        for a, step_k, base in (("H", 1, 17), ("L", -1, 16)):
+            cnt_i = const.tile([P, P], I32, name="cnt_i" + a)
+            nc.gpsimd.iota(cnt_i[:], pattern=[[0, B], [step_k, 16]], base=base, channel_multiplier=0)
+            cnt[a] = const.tile([P, P], BF16, name="cnt" + a)
+            nc.vector.memset(cnt[a][:], 0.0)
+            nc.vector.tensor_scalar(out=cnt[a][32:33, :], in0=cnt_i[32:33, :], scalar1=1.0 / 32.0, scalar2=None, op0=ALU.mult)
 
         xw = x_sb[:].bitcast(F32)
         xg = const.tile([P, 2048], BF16, name="xg", align_bytes=64)
         xgw = xg[:].bitcast(F32)
         for g in range(2):
-            xt = psum.tile([P, 2, 2, P], F32, name="xt%d" % g, tag="y%d" % g)
+            xt = psum.tile([P, 2, 2, P], F32, name="xt%d" % g, tag="p%s0" % "ab"[g])
             for h in range(2):
                 for u in range(2):
                     col = 512 * h + 256 * g + 128 * u
@@ -179,13 +165,12 @@ def tile_causalexpert_pa_t_kernel(tc, x_attn, cw1, cb1, cw2, cb2, cln_g, cln_b, 
             )
 
         a_pos = const.tile([P, B, 32, 4], F32, name="a_pos")
-        a_low = const.tile([P, B, 16, 4], F32, name="a_low")
         eT = const.tile([P, 256, 4], F32, name="eT")
         ps1 = {}
 
         def first_mm(half):
             for h in range(2):
-                ps1[(half, h)] = psum.tile([P, 4, P], F32, name="ps1_%d%d" % (half, h), tag=(("y2", "y3"), ("pa0", "pb0"))[half][h])
+                ps1[(half, h)] = psum.tile([P, 4, P], F32, name="ps1_%d%d" % (half, h), tag="ye"[half] + str(h))
                 for t2 in range(4):
                     for g in range(2):
                         wc = 512 * (2 * half + g) + 128 * t2
@@ -203,42 +188,39 @@ def tile_causalexpert_pa_t_kernel(tc, x_attn, cw1, cb1, cw2, cb2, cln_g, cln_b, 
         regroup1("v", 0)
         regroup1("s", 1)
         nc.vector.quantize_mx(out=xq[:].bitcast(FP8X4), scales=xs[:], in_=xg[:])
-        regroup1("v", 2)
         quant1(0)
+        sm_ps = psum.tile([P, P], BF16, name="sm_ps", tag="pa1")
+        nc.tensor.transpose(sm_ps[:], sm[:], ident_b[:])
+        smT = const.tile([P, 12], F32, name="smT")
+        nc.vector.tensor_copy(out=smT[:], in_=sm_ps[:, 0:12])
+        regroup1("v", 2)
         quant1(1)
         first_mm(0)
-        regroup1("v", 3)
+        regroup1("s", 3)
         quant1(2)
         quant1(3)
         first_mm(1)
-        regroup("s", w2g[0][:], raw2[:, :, 0:512])
         bias = smT[:, 8:12].unsqueeze(1).unsqueeze(1).to_broadcast([P, 4, 16, 4])
-        for h in range(2):
-            src4 = ps1[(0, h)][:].rearrange("p t (b i) -> p b i t", b=4)
-            nc.vector.tensor_tensor(out=a_pos[:, 4 * h : 4 * h + 4, 0:16, :], in0=src4[:, :, 16:32, :], in1=bias, op=ALU.add)
-        for h in range(2):
-            src4 = ps1[(0, h)][:].rearrange("p t (b i) -> p b i t", b=4)
-            nc.vector.tensor_tensor(out=a_low[:, 4 * h : 4 * h + 4, :, :], in0=src4[:, :, 0:16, :], in1=bias, op=ALU.add)
-        for h in range(2):
-            nc.scalar.copy(out=eT[:, 128 * h : 128 * h + 128, :], in_=ps1[(1, h)][:].rearrange("p t r -> p r t"))
-        for k in range(16):
-            nc.scalar.copy(out=a_pos[:, :, 16 + k, :], in_=a_low[:, :, 15 - k, :])
-        regroup("v", w2g[1][:], raw2[:, :, 512:1024])
-        quant2(0)
-        quant2(1)
+        for lo in range(2):
+            for h in range(2):
+                src4 = ps1[(0, h)][:].rearrange("p t (b i) -> p b i t", b=4)
+                part = src4[:, :, 0:16, :][:, :, ::-1, :] if lo else src4[:, :, 16:32, :]
+                nc.vector.tensor_tensor(out=a_pos[:, 4 * h : 4 * h + 4, 16 * lo : 16 * lo + 16, :], in0=part, in1=bias, op=ALU.add)
+        e_ps = [ps1[(1, h)][:].rearrange("p t (b i) -> p b i t", b=4) for h in range(2)]
         e4 = eT[:].rearrange("p (b i) t -> p b i t", b=B)
 
-        ssum = const.tile([P, 2 * n_tiles], F32, name="ssum")
-        nm = const.tile([P, n_tiles], F32, name="nm")
-        ssq = const.tile([P, n_tiles], F32, name="ssq")
-        tv = const.tile([P, n_tiles], F32, name="tv")
-        wv = const.tile([P, n_tiles], F32, name="wv")
-        nmw = const.tile([P, n_tiles], F32, name="nmw")
+        ssum = const.tile([P, 2 * N_TILES], F32, name="ssum")
+        nm = const.tile([P, N_TILES], F32, name="nm")
+        ssq = const.tile([P, N_TILES], F32, name="ssq")
+        tv = const.tile([P, N_TILES], F32, name="tv")
+        wv = const.tile([P, N_TILES], F32, name="wv")
+        nmw = const.tile([P, N_TILES], F32, name="nmw")
+        hq = const.tile([P, P * N_TILES], U32, name="hq", align_bytes=64)
+        hs = const.tile([P, P * N_TILES], U8, name="hs", align_bytes=64)
 
         acc = {}
         hp_t = {}
         h2_t = {}
-        hq_t = {}
         yps_t = {}
         y_t = {}
         z_t = {}
@@ -246,41 +228,49 @@ def tile_causalexpert_pa_t_kernel(tc, x_attn, cw1, cb1, cw2, cb2, cln_g, cln_b, 
 
         def stage_add(g):
             t0, n = groups[g]
-            hp_t[g] = hp_pool.tile([P, 512 * gmax], F32, name="hp")
+            hp_t[g] = hp_pool.tile([P, 1024], F32, name="hp")
             for ti in range(n):
                 view = hp_t[g][:, 512 * ti : 512 * ti + 512].rearrange("p (b s t) -> p b s t", b=B, t=4)
                 w, parts = tiles[t0 + ti]
                 for s0, ns, j in parts:
-                    nc.vector.tensor_tensor(
-                        out=view[:, :, s0 : s0 + ns, :],
-                        in0=a_pos[:, :, w + s0 : w + s0 + ns, :],
-                        in1=e4[:, :, j : j + 1, :].to_broadcast([P, B, ns, 4]),
-                        op=ALU.add,
-                    )
+                    if t0 + ti in G_ADDS:
+                        nc.gpsimd.tensor_tensor(
+                            out=view[:, :, s0 : s0 + ns, :],
+                            in0=a_pos[:, :, w + s0 : w + s0 + ns, :],
+                            in1=e4[:, :, j : j + 1, :].to_broadcast([P, B, ns, 4]),
+                            op=ALU.add,
+                        )
+                    else:
+                        for h in range(2):
+                            nc.vector.tensor_tensor(
+                                out=view[:, 4 * h : 4 * h + 4, s0 : s0 + ns, :],
+                                in0=a_pos[:, 4 * h : 4 * h + 4, w + s0 : w + s0 + ns, :],
+                                in1=e_ps[h][:, :, j : j + 1, :].to_broadcast([P, 4, ns, 4]),
+                                op=ALU.add,
+                            )
 
         def stage_gelu(g):
             n = groups[g][1]
-            h2_t[g] = h2_pool.tile([P, 512 * gmax], BF16, name="h2", align_bytes=64)
+            h2_t[g] = h2_pool.tile([P, 1024], BF16, name="h2", align_bytes=64)
             nc.scalar.activation(out=h2_t[g][:, 0 : 512 * n], in_=hp_t[g][:, 0 : 512 * n], func=ACT.Gelu)
 
         def stage_quant(g):
-            n = groups[g][1]
-            hq = hq_pool.tile([P, 128 * gmax], U32, name="hq", align_bytes=64)
-            hs = hq_pool.tile([P, 128 * gmax], U8, name="hs", align_bytes=64)
-            hq_t[g] = (hq, hs)
-            nc.vector.quantize_mx(out=hq[:, 0 : 128 * n].bitcast(FP8X4), scales=hs[:, 0 : 128 * n], in_=h2_t[g][:, 0 : 512 * n])
+            t0, n = groups[g]
+            sl = slice(P * t0, P * (t0 + n))
+            nc.vector.quantize_mx(out=hq[:, sl].bitcast(FP8X4), scales=hs[:, sl], in_=h2_t[g][:, 0 : 512 * n])
 
         def stage_mm(t):
-            g = group_of[t]
-            ti = t - groups[g][0]
-            hq, hs = hq_t[g]
             for hf in range(2):
-                yps_t[(t, hf)] = psum.tile([P, 512], F32, name="yps", tag="y%d" % (2 * (t % 2) + hf))
-                for rep in range(1 + (DUP if hf == 0 else 0)):
+                if t < T_WIDE:
+                    tag = "y%d" % hf
+                else:
+                    tag = "ye"[t % 2] + str(hf)
+                yps_t[(t, hf)] = psum.tile([P, 512], F32, name="yps", tag=tag)
+                for rep in range(1 + (DUP if hf == 0 and t < T_WIDE else 0)):
                     nc.tensor.matmul_mx(
                         out=yps_t[(t, hf)][:],
-                        lhsT=hq[:, 128 * ti : 128 * ti + 128].bitcast(FP8X4),
-                        lhsT_scale=hs[:, 128 * ti : 128 * ti + 128],
+                        lhsT=hq[:, P * t : P * t + P].bitcast(FP8X4),
+                        lhsT_scale=hs[:, P * t : P * t + P],
                         rhs=w2q[:, 512 * hf : 512 * hf + 512].bitcast(FP8X4),
                         rhs_scale=w2s[:, 512 * hf : 512 * hf + 512],
                         start=True,
@@ -299,40 +289,35 @@ def tile_causalexpert_pa_t_kernel(tc, x_attn, cw1, cb1, cw2, cb2, cln_g, cln_b, 
                     op1=ALU.add,
                     accum_out=ssum[:, 2 * t + hf : 2 * t + hf + 1],
                 )
-            nc.vector.tensor_scalar(
-                out=nm[:, t : t + 1],
-                in0=ssum[:, 2 * t : 2 * t + 1],
-                scalar1=ssum[:, 2 * t + 1 : 2 * t + 2],
-                scalar2=-1.0 / D,
-                op0=ALU.add,
-                op1=ALU.mult,
-            )
 
         def stage_square(t):
+            scaled = junk_pool.tile([P, 2], F32, name="scaled")
+            nc.scalar.activation(out=scaled[:], in_=ssum[:, 2 * t : 2 * t + 2], func=ACT.Identity, scale=-1.0 / D, accum_out=nm[:, t : t + 1])
             junk = junk_pool.tile([P, 1024], BF16, name="junk")
             nc.scalar.activation(out=junk[:], in_=y_t[t][:], func=ACT.Square, bias=nm[:, t : t + 1], scale=1.0, accum_out=ssq[:, t : t + 1])
 
-        def stage_weight(g):
-            t0, n = groups[g]
-            sl = slice(t0, t0 + n)
+        def stage_weight_g(ta, n):
+            sl = slice(ta, ta + n)
             nc.gpsimd.tensor_scalar(out=tv[:, sl], in0=ssq[:, sl], scalar1=1.0, scalar2=D * EPS, op0=ALU.mult, op1=ALU.add)
             nc.gpsimd.tensor_tensor(out=wv[:, sl], in0=tv[:, sl], in1=mhalf[:, 0:n], op=ALU.pow)
-            if any(z_engine(t) == "s" for t in range(t0, t0 + n)):
-                nc.gpsimd.tensor_tensor(out=nmw[:, sl], in0=nm[:, sl], in1=wv[:, sl], op=ALU.mult)
+
+        def stage_weight_s(t):
+            nc.scalar.activation(out=wv[:, t : t + 1], in_=ssq[:, t : t + 1], func=ACT.Abs_reciprocal_sqrt, bias=deps[:], scale=1.0)
 
         def stage_z(t):
             z_t[t] = z_pool.tile([P, 1024], F32, name="z")
-            eng = z_engine(t)
-            if eng == "s":
-                nc.scalar.activation(out=z_t[t][:], in_=y_t[t][:], func=ACT.Identity, bias=nmw[:, t : t + 1], scale=wv[:, t : t + 1])
-            elif eng == "g":
-                nc.gpsimd.tensor_scalar(
-                    out=z_t[t][:], in0=y_t[t][:], scalar1=nm[:, t : t + 1], scalar2=wv[:, t : t + 1], op0=ALU.add, op1=ALU.mult
-                )
-            else:
-                nc.vector.tensor_scalar(
-                    out=z_t[t][:], in0=y_t[t][:], scalar1=nm[:, t : t + 1], scalar2=wv[:, t : t + 1], op0=ALU.add, op1=ALU.mult
-                )
+            eng = z_engines(t)
+            wd = 1024 // len(eng)
+            for k in range(len(eng)):
+                sl = slice(wd * k, wd * k + wd)
+                if eng[k] == "a":
+                    nc.scalar.activation(out=nmw[:, t : t + 1], in_=nm[:, t : t + 1], func=ACT.Copy, scale=wv[:, t : t + 1])
+                    nc.scalar.activation(out=z_t[t][:, sl], in_=y_t[t][:, sl], func=ACT.Identity, bias=nmw[:, t : t + 1], scale=wv[:, t : t + 1])
+                else:
+                    engine = nc.gpsimd if eng[k] == "g" else nc.vector
+                    engine.tensor_scalar(
+                        out=z_t[t][:, sl], in0=y_t[t][:, sl], scalar1=nm[:, t : t + 1], scalar2=wv[:, t : t + 1], op0=ALU.add, op1=ALU.mult
+                    )
 
         def stage_sum(t):
             w = tiles[t][0]
@@ -350,7 +335,7 @@ def tile_causalexpert_pa_t_kernel(tc, x_attn, cw1, cb1, cw2, cb2, cln_g, cln_b, 
                         acc[key] = psum.tile([P, 4, B, 16], F32, name="acc2_%d" % (c // 4), tag="pa%d" % (c // 4))
                     dst = acc[key][:, c % 4, :, :]
                     first = t == N_PHASE1 and c % 4 == 0
-                    last = t == n_tiles - 1 and c % 4 == 3
+                    last = t == N_TILES - 1 and c % 4 == 3
                 nc.tensor.matmul(dst, lhsT=z_t[t][:, 128 * c : 128 * c + 128], rhs=ident3, is_transpose=True, start=first, stop=last)
 
         oT = {}
@@ -371,20 +356,23 @@ def tile_causalexpert_pa_t_kernel(tc, x_attn, cw1, cb1, cw2, cb2, cln_g, cln_b, 
                         out=oT[a][:, c, :, :], in_=acc[(1, c // 2)][:, c % 2, :, p0 : p0 + 16], func=ACT.Copy, scale=smT[:, c : c + 1]
                     )
 
-        def stage_back(a, sources, opens, closes):
+        def back_open(a):
             for hb in range(2):
-                if opens:
-                    back[(a, hb)] = psum.tile([P, 512], F32, name="back%s%d" % (a, hb), tag="pb%d" % hb)
-                for n_src, src in enumerate(sources):
-                    for c in range(4):
-                        nc.tensor.matmul(
-                            back[(a, hb)][:, 128 * c : 128 * c + 128],
-                            lhsT=src[:, 4 * hb + c, :],
-                            rhs=ident_f[:],
-                            is_transpose=True,
-                            start=(opens and n_src == 0 and c == 0),
-                            stop=(closes and n_src == len(sources) - 1 and c == 3),
-                        )
+                back[(a, hb)] = psum.tile([P, 512], F32, name="back%s%d" % (a, hb), tag="pb%d" % hb)
+                nc.tensor.matmul(back[(a, hb)][:], lhsT=cnt[a][:], rhs=rows[:, 512 * hb : 512 * hb + 512], start=True, stop=False)
+
+        def back_add(a, src, closes):
+            flat = src[:].rearrange("p c b s -> p c (b s)")
+            for hb in range(2):
+                for c in range(4):
+                    nc.tensor.matmul(
+                        back[(a, hb)][:, 128 * c : 128 * c + 128],
+                        lhsT=flat[:, 4 * hb + c, :],
+                        rhs=ident_f[:],
+                        is_transpose=True,
+                        start=False,
+                        stop=(closes and c == 3),
+                    )
 
         def stage_last():
             gain = smT[:, 0:4].unsqueeze(2).to_broadcast([P, 4, P])
@@ -405,34 +393,57 @@ def tile_causalexpert_pa_t_kernel(tc, x_attn, cw1, cb1, cw2, cb2, cln_g, cln_b, 
                 for k in range(16):
                     nc.sync.dma_start(out=out[:, 15 - k, :], in_=osb[k : P : 16, :])
 
-        def flat(tile_ap):
-            return tile_ap.rearrange("p c b s -> p c (b s)")
+        stage_add(0)
+        regroup("s", w2g[0][:], raw2[:, :, 0:512])
+        stage_gelu(0)
+        cb2_bc = const.tile([P, 1024], F32, name="cb2_bc")
+        cb_ps = []
+        for hf in range(2):
+            cb_ps.append(psum.tile([P, 512], F32, name="cb_ps%d" % hf, tag="p%s1" % "ab"[hf]))
+            nc.tensor.matmul(cb_ps[hf][:], lhsT=pick0[:], rhs=rows[:, 512 * hf : 512 * hf + 512], start=True, stop=True)
+        regroup("v", w2g[1][:], raw2[:, :, 512:1024])
+        quant2(0)
+        for h in range(2):
+            nc.scalar.copy(out=eT[:, 128 * h : 128 * h + 128, :], in_=ps1[(1, h)][:].rearrange("p t r -> p r t"))
+        stage_quant(0)
+        stage_add(1)
+        quant2(1)
+        stage_mm(0)
+        for hf in range(2):
+            nc.scalar.copy(out=cb2_bc[:, 512 * hf : 512 * hf + 512], in_=cb_ps[hf][:])
+        stage_gelu(1)
+        stage_add(2)
 
-        for step in range(-LAG_ADD, n_tiles + LAG_SUM):
-            if step + LAG_ADD in first_of:
-                stage_add(first_of[step + LAG_ADD])
-            if step + LAG_GELU in first_of:
-                stage_gelu(first_of[step + LAG_GELU])
-            if 0 <= step + 1 < n_tiles:
-                stage_mm(step + 1)
-            if 0 <= step < n_tiles:
+        for step in range(0, N_TILES + LAG_SUM):
+            if step + 2 < n_groups:
+                stage_gelu(step + 2)
+            if step < N_TILES:
                 stage_bias(step)
                 stage_square(step)
-            if step + LAG_QUANT in first_of:
-                stage_quant(first_of[step + LAG_QUANT])
-            if step in last_of:
-                stage_weight(last_of[step])
-            if 0 <= step - LAG_Z < n_tiles:
+            if step + 1 < n_groups:
+                stage_quant(step + 1)
+            if step + 1 < N_TILES:
+                stage_mm(step + 1)
+            if step + LEAD < n_groups:
+                stage_add(step + LEAD)
+            tw = step - LAG_Z
+            if 0 <= tw < T_RSQ and tw % 2 == 0:
+                stage_weight_g(tw, 2)
+            if T_RSQ <= step - 1 < N_TILES:
+                stage_weight_s(step - 1)
+            if 0 <= step - LAG_Z < N_TILES:
                 stage_z(step - LAG_Z)
-            if 0 <= step - LAG_SUM < n_tiles:
+            if 0 <= step - LAG_SUM < N_TILES:
                 stage_sum(step - LAG_SUM)
             if step - LAG_SUM == N_PHASE1 - 1:
                 stage_mid()
             if step - LAG_SUM == N_PHASE1 + 1:
-                stage_back("L", [bcT["L"][:], flat(oT["L"][:])], True, True)
+                back_open("L")
+                back_add("L", oT["L"], True)
                 stage_store("L")
             if step - LAG_SUM == N_PHASE1 + 3:
-                stage_back("H", [bcT["H"][:], flat(oT["H1"][:])], True, False)
+                back_open("H")
+                back_add("H", oT["H1"], False)
         stage_last()
-        stage_back("H", [flat(oT["H2"][:])], False, True)
+        back_add("H", oT["H2"], True)
         stage_store("H")

@@ -19,13 +19,10 @@ FLOPS = 2 * (B * L) * (2 * D) * C + 2 * (B * L * (L + 1) // 2) * C * D
 
 N_PHASE1 = 17
 N_TILES = 33
-GROUPS = [1] + [2] * 16
-LEAD = 3
-T_WIDE = 15
-T_RSQ = 16
+GROUPS = [1, 2, 2] + [4] * 7
 LAG_Z, LAG_SUM = 2, 4
-G_ADDS = (2, 6, 10, 14, 18, 22, 26, 30)
-DUP = 1
+LAG_SUM2 = 6
+G_ADDS = (4, 7, 8, 12, 15, 16, 20, 23, 24, 28, 32)
 
 
 def z_engines(t):
@@ -61,10 +58,10 @@ def tile_causalexpert_pa_t_kernel(tc, x_attn, cw1, cb1, cw2, cb2, cln_g, cln_b, 
 
     with ExitStack() as ctx:
         const = ctx.enter_context(tc.tile_pool(name="const", bufs=1))
-        hp_pool = ctx.enter_context(tc.tile_pool(name="hp", bufs=4))
+        hp_pool = ctx.enter_context(tc.tile_pool(name="hp", bufs=3))
         h2_pool = ctx.enter_context(tc.tile_pool(name="h2", bufs=3))
         y_pool = ctx.enter_context(tc.tile_pool(name="y", bufs=8))
-        z_pool = ctx.enter_context(tc.tile_pool(name="z", bufs=6))
+        z_pool = ctx.enter_context(tc.tile_pool(name="z", bufs=8))
         junk_pool = ctx.enter_context(tc.tile_pool(name="junk", bufs=2))
         psum = ctx.enter_context(tc.psum_pool(name="psum", bufs=1))
         ctx.enter_context(tc.manual_schedule())
@@ -102,8 +99,6 @@ def tile_causalexpert_pa_t_kernel(tc, x_attn, cw1, cb1, cw2, cb2, cln_g, cln_b, 
         pick0 = const.tile([P, P], BF16, name="pick0")
         nc.vector.memset(pick0[:], 0.0)
         nc.vector.memset(pick0[0:1, :], 1.0)
-        mhalf = const.tile([P, 4], F32, name="mhalf")
-        nc.vector.memset(mhalf[:], -0.5)
         deps = const.tile([P, 1], F32, name="deps")
         nc.vector.tensor_scalar(out=deps[:], in0=warm[:, 0:1], scalar1=1.0, scalar2=D * EPS, op0=ALU.mult, op1=ALU.add)
         cnt = {}
@@ -212,7 +207,6 @@ def tile_causalexpert_pa_t_kernel(tc, x_attn, cw1, cb1, cw2, cb2, cln_g, cln_b, 
         ssum = const.tile([P, 2 * N_TILES], F32, name="ssum")
         nm = const.tile([P, N_TILES], F32, name="nm")
         ssq = const.tile([P, N_TILES], F32, name="ssq")
-        tv = const.tile([P, N_TILES], F32, name="tv")
         wv = const.tile([P, N_TILES], F32, name="wv")
         nmw = const.tile([P, N_TILES], F32, name="nmw")
         hq = const.tile([P, P * N_TILES], U32, name="hq", align_bytes=64)
@@ -228,7 +222,7 @@ def tile_causalexpert_pa_t_kernel(tc, x_attn, cw1, cb1, cw2, cb2, cln_g, cln_b, 
 
         def stage_add(g):
             t0, n = groups[g]
-            hp_t[g] = hp_pool.tile([P, 1024], F32, name="hp")
+            hp_t[g] = hp_pool.tile([P, 2048], F32, name="hp")
             for ti in range(n):
                 view = hp_t[g][:, 512 * ti : 512 * ti + 512].rearrange("p (b s t) -> p b s t", b=B, t=4)
                 w, parts = tiles[t0 + ti]
@@ -251,7 +245,7 @@ def tile_causalexpert_pa_t_kernel(tc, x_attn, cw1, cb1, cw2, cb2, cln_g, cln_b, 
 
         def stage_gelu(g):
             n = groups[g][1]
-            h2_t[g] = h2_pool.tile([P, 1024], BF16, name="h2", align_bytes=64)
+            h2_t[g] = h2_pool.tile([P, 2048], BF16, name="h2", align_bytes=64)
             nc.scalar.activation(out=h2_t[g][:, 0 : 512 * n], in_=hp_t[g][:, 0 : 512 * n], func=ACT.Gelu)
 
         def stage_quant(g):
@@ -261,21 +255,16 @@ def tile_causalexpert_pa_t_kernel(tc, x_attn, cw1, cb1, cw2, cb2, cln_g, cln_b, 
 
         def stage_mm(t):
             for hf in range(2):
-                if t < T_WIDE:
-                    tag = "y%d" % hf
-                else:
-                    tag = "ye"[t % 2] + str(hf)
-                yps_t[(t, hf)] = psum.tile([P, 512], F32, name="yps", tag=tag)
-                for rep in range(1 + (DUP if hf == 0 and t < T_WIDE else 0)):
-                    nc.tensor.matmul_mx(
-                        out=yps_t[(t, hf)][:],
-                        lhsT=hq[:, P * t : P * t + P].bitcast(FP8X4),
-                        lhsT_scale=hs[:, P * t : P * t + P],
-                        rhs=w2q[:, 512 * hf : 512 * hf + 512].bitcast(FP8X4),
-                        rhs_scale=w2s[:, 512 * hf : 512 * hf + 512],
-                        start=True,
-                        stop=True,
-                    )
+                yps_t[(t, hf)] = psum.tile([P, 512], F32, name="yps", tag="ye"[t % 2] + str(hf))
+                nc.tensor.matmul_mx(
+                    out=yps_t[(t, hf)][:],
+                    lhsT=hq[:, P * t : P * t + P].bitcast(FP8X4),
+                    lhsT_scale=hs[:, P * t : P * t + P],
+                    rhs=w2q[:, 512 * hf : 512 * hf + 512].bitcast(FP8X4),
+                    rhs_scale=w2s[:, 512 * hf : 512 * hf + 512],
+                    start=True,
+                    stop=True,
+                )
 
         def stage_bias(t):
             y_t[t] = y_pool.tile([P, 1024], F32, name="y")
@@ -290,18 +279,15 @@ def tile_causalexpert_pa_t_kernel(tc, x_attn, cw1, cb1, cw2, cb2, cln_g, cln_b, 
                     accum_out=ssum[:, 2 * t + hf : 2 * t + hf + 1],
                 )
 
-        def stage_square(t):
+        def stage_nm(t):
             scaled = junk_pool.tile([P, 2], F32, name="scaled")
             nc.scalar.activation(out=scaled[:], in_=ssum[:, 2 * t : 2 * t + 2], func=ACT.Identity, scale=-1.0 / D, accum_out=nm[:, t : t + 1])
+
+        def stage_square(t):
             junk = junk_pool.tile([P, 1024], BF16, name="junk")
             nc.scalar.activation(out=junk[:], in_=y_t[t][:], func=ACT.Square, bias=nm[:, t : t + 1], scale=1.0, accum_out=ssq[:, t : t + 1])
 
-        def stage_weight_g(ta, n):
-            sl = slice(ta, ta + n)
-            nc.gpsimd.tensor_scalar(out=tv[:, sl], in0=ssq[:, sl], scalar1=1.0, scalar2=D * EPS, op0=ALU.mult, op1=ALU.add)
-            nc.gpsimd.tensor_tensor(out=wv[:, sl], in0=tv[:, sl], in1=mhalf[:, 0:n], op=ALU.pow)
-
-        def stage_weight_s(t):
+        def stage_weight(t):
             nc.scalar.activation(out=wv[:, t : t + 1], in_=ssq[:, t : t + 1], func=ACT.Abs_reciprocal_sqrt, bias=deps[:], scale=1.0)
 
         def stage_z(t):
@@ -393,55 +379,58 @@ def tile_causalexpert_pa_t_kernel(tc, x_attn, cw1, cb1, cw2, cb2, cln_g, cln_b, 
                 for k in range(16):
                     nc.sync.dma_start(out=out[:, 15 - k, :], in_=osb[k : P : 16, :])
 
+        for h in range(2):
+            nc.scalar.copy(out=eT[:, 128 * h : 128 * h + 128, :], in_=ps1[(1, h)][:].rearrange("p t r -> p r t"))
         stage_add(0)
-        regroup("s", w2g[0][:], raw2[:, :, 0:512])
+        stage_add(1)
         stage_gelu(0)
         cb2_bc = const.tile([P, 1024], F32, name="cb2_bc")
         cb_ps = []
         for hf in range(2):
             cb_ps.append(psum.tile([P, 512], F32, name="cb_ps%d" % hf, tag="p%s1" % "ab"[hf]))
             nc.tensor.matmul(cb_ps[hf][:], lhsT=pick0[:], rhs=rows[:, 512 * hf : 512 * hf + 512], start=True, stop=True)
-        regroup("v", w2g[1][:], raw2[:, :, 512:1024])
-        quant2(0)
-        for h in range(2):
-            nc.scalar.copy(out=eT[:, 128 * h : 128 * h + 128, :], in_=ps1[(1, h)][:].rearrange("p t r -> p r t"))
-        stage_quant(0)
-        stage_add(1)
-        quant2(1)
+        for g in range(2, n_groups):
+            stage_add(g)
+            if g == 3:
+                for hf in range(2):
+                    nc.scalar.copy(out=cb2_bc[:, 512 * hf : 512 * hf + 512], in_=cb_ps[hf][:])
+            if g in (4, 6):
+                hf = (g - 4) // 2
+                regroup("v", w2g[hf][:], raw2[:, :, 512 * hf : 512 * hf + 512])
+            if g in (5, 7):
+                quant2((g - 5) // 2)
+            stage_gelu(g - 1)
+            stage_quant(g - 2)
+        stage_gelu(n_groups - 1)
         stage_mm(0)
-        for hf in range(2):
-            nc.scalar.copy(out=cb2_bc[:, 512 * hf : 512 * hf + 512], in_=cb_ps[hf][:])
-        stage_gelu(1)
-        stage_add(2)
+        stage_mm(1)
 
-        for step in range(0, N_TILES + LAG_SUM):
-            if step + 2 < n_groups:
-                stage_gelu(step + 2)
+        for step in range(0, N_TILES + LAG_SUM2):
             if step < N_TILES:
                 stage_bias(step)
+                stage_nm(step)
+            if 0 <= step - 1 < N_TILES:
+                stage_weight(step - 1)
+            if step < N_TILES:
                 stage_square(step)
-            if step + 1 < n_groups:
-                stage_quant(step + 1)
-            if step + 1 < N_TILES:
-                stage_mm(step + 1)
-            if step + LEAD < n_groups:
-                stage_add(step + LEAD)
-            tw = step - LAG_Z
-            if 0 <= tw < T_RSQ and tw % 2 == 0:
-                stage_weight_g(tw, 2)
-            if T_RSQ <= step - 1 < N_TILES:
-                stage_weight_s(step - 1)
+            if step in (1, 2):
+                stage_quant(n_groups - 3 + step)
+            if step + 2 < N_TILES:
+                stage_mm(step + 2)
             if 0 <= step - LAG_Z < N_TILES:
                 stage_z(step - LAG_Z)
-            if 0 <= step - LAG_SUM < N_TILES:
-                stage_sum(step - LAG_SUM)
-            if step - LAG_SUM == N_PHASE1 - 1:
+            if step - LAG_SUM == N_PHASE1:
                 stage_mid()
-            if step - LAG_SUM == N_PHASE1 + 1:
+            if 0 <= step - LAG_SUM < N_PHASE1:
+                stage_sum(step - LAG_SUM)
+            if N_PHASE1 <= step - LAG_SUM2 < N_TILES:
+                stage_sum(step - LAG_SUM2)
+            if step - LAG_SUM2 == N_PHASE1:
                 back_open("L")
                 back_add("L", oT["L"], True)
+            if step - LAG_SUM2 == N_PHASE1 + 2:
                 stage_store("L")
-            if step - LAG_SUM == N_PHASE1 + 3:
+            if step - LAG_SUM2 == N_PHASE1 + 4:
                 back_open("H")
                 back_add("H", oT["H1"], False)
         stage_last()

@@ -20,17 +20,12 @@ FLOPS = 2 * (B * L) * (2 * D) * C + 2 * (B * L * (L + 1) // 2) * C * D
 N_PHASE1 = 17
 N_TILES = 33
 GROUPS = [1, 2, 2] + [4] * 7
-LAG_Z, LAG_SUM = 2, 4
-LAG_SUM2 = 6
-G_ADDS = (4, 7, 8, 12, 15, 16, 20, 23, 24, 28, 32)
+QUANTS = [(0, 1), (1, 8), (9, 8), (17, 8), (25, 8)]
+G_ADDS = (4, 7, 8, 12, 15, 16, 20, 23, 24, 28)
 
 
 def z_engines(t):
-    if t == N_TILES - 1:
-        return "va"
-    if t == N_TILES - 2:
-        return "gv"
-    return "g"
+    return "v" if t > N_TILES - 5 else "g"
 
 
 def tile_parts():
@@ -58,143 +53,145 @@ def tile_causalexpert_pa_t_kernel(tc, x_attn, cw1, cb1, cw2, cb2, cln_g, cln_b, 
 
     with ExitStack() as ctx:
         const = ctx.enter_context(tc.tile_pool(name="const", bufs=1))
-        hp_pool = ctx.enter_context(tc.tile_pool(name="hp", bufs=3))
-        h2_pool = ctx.enter_context(tc.tile_pool(name="h2", bufs=3))
-        y_pool = ctx.enter_context(tc.tile_pool(name="y", bufs=8))
-        z_pool = ctx.enter_context(tc.tile_pool(name="z", bufs=8))
+        hp_pool = ctx.enter_context(tc.tile_pool(name="hp", bufs=4))
         junk_pool = ctx.enter_context(tc.tile_pool(name="junk", bufs=2))
         psum = ctx.enter_context(tc.psum_pool(name="psum", bufs=1))
         ctx.enter_context(tc.manual_schedule())
 
-        x_sb = const.tile([P, 2048], BF16, name="x_sb")
-        nc.sync.dma_start(
-            out=x_sb[:].rearrange("p (h d) -> p h d", h=2),
-            in_=x_attn.flatten_outer_dims().rearrange("(h p) d -> p h d", p=P),
-        )
-        raw1 = const.tile([P, 8, 1024], BF16, name="raw1")
-        w1_view = cw1.rearrange("(s q e) c -> q s (e c)", s=8, q=P, e=2)
-        for unit in range(4):
-            nc.sync.dma_start(out=raw1[:, 2 * unit : 2 * unit + 2, :], in_=w1_view[:, 2 * unit : 2 * unit + 2, :])
-        raw2 = const.tile([P, 4, 1024], BF16, name="raw2")
-        w2_view = cw2.rearrange("(t p) n -> p t n", p=P)
-        for hf in range(2):
-            nc.sync.dma_start(out=raw2[:, :, 512 * hf : 512 * hf + 512], in_=w2_view[:, :, 512 * hf : 512 * hf + 512])
-
-        ident_f = const.tile([P, P], F32, name="ident_f")
-        make_identity(nc, ident_f[:])
-        sm = const.tile([P, P], BF16, name="sm")
-        nc.vector.memset(sm[:], 0.0)
-        rows = const.tile([P, 1024], BF16, name="rows")
-        nc.vector.memset(rows[:], 0.0)
-        nc.scalar.dma_start(out=sm[0:8, :], in_=cln_g.rearrange("(c p) -> c p", p=P))
-        nc.scalar.dma_start(out=sm[8:12, :], in_=cb1.rearrange("(t p) -> t p", p=P))
-        nc.scalar.dma_start(out=rows[0:1, :], in_=cb2.rearrange("(o n) -> o n", o=1))
-        nc.scalar.dma_start(out=rows[32:33, :], in_=cln_b.rearrange("(o n) -> o n", o=1))
-        warm = const.tile([P, 2], F32, name="warm")
-        nc.vector.memset(warm[:], 0.0)
-        warm_o = const.tile([P, 2], BF16, name="warm_o")
-        nc.scalar.activation(out=warm_o[:], in_=warm[:], func=ACT.Gelu)
-        ident_b = const.tile([P, P], BF16, name="ident_b")
-        nc.vector.tensor_copy(out=ident_b[:], in_=ident_f[:])
-        pick0 = const.tile([P, P], BF16, name="pick0")
-        nc.vector.memset(pick0[:], 0.0)
-        nc.vector.memset(pick0[0:1, :], 1.0)
-        deps = const.tile([P, 1], F32, name="deps")
-        nc.vector.tensor_scalar(out=deps[:], in0=warm[:, 0:1], scalar1=1.0, scalar2=D * EPS, op0=ALU.mult, op1=ALU.add)
-        cnt = {}
-        for a, step_k, base in (("H", 1, 17), ("L", -1, 16)):
-            cnt_i = const.tile([P, P], I32, name="cnt_i" + a)
-            nc.gpsimd.iota(cnt_i[:], pattern=[[0, B], [step_k, 16]], base=base, channel_multiplier=0)
-            cnt[a] = const.tile([P, P], BF16, name="cnt" + a)
-            nc.vector.memset(cnt[a][:], 0.0)
-            nc.vector.tensor_scalar(out=cnt[a][32:33, :], in0=cnt_i[32:33, :], scalar1=1.0 / 32.0, scalar2=None, op0=ALU.mult)
-
-        xw = x_sb[:].bitcast(F32)
-        xg = const.tile([P, 2048], BF16, name="xg", align_bytes=64)
-        xgw = xg[:].bitcast(F32)
-        for g in range(2):
-            xt = psum.tile([P, 2, 2, P], F32, name="xt%d" % g, tag="p%s0" % "ab"[g])
-            for h in range(2):
-                for u in range(2):
-                    col = 512 * h + 256 * g + 128 * u
-                    nc.tensor.transpose(xt[:, h, u, :], xw[:, col : col + 128], ident_f[:])
-            dst = xgw[:, 512 * g : 512 * g + 512].rearrange("p (h r u) -> p h r u", h=2, u=2)
-            src = xt[:].rearrange("p h u r -> p h r u")
-            if g == 0:
-                nc.vector.tensor_copy(out=dst, in_=src)
-            else:
-                nc.scalar.copy(out=dst, in_=src)
-        xq = const.tile([P, 512], U32, name="xq", align_bytes=64)
-        xs = const.tile([P, 512], U8, name="xs", align_bytes=64)
-
-        def regroup(engine, dst, src):
-            d = dst.rearrange("p (c i) t -> p c t i", i=4)
-            s = src.rearrange("p t (c i) -> p c t i", i=4)
-            if engine == "v":
-                nc.vector.tensor_copy(out=d, in_=s)
-            else:
-                nc.scalar.copy(out=d, in_=s)
-
-        w1q = const.tile([P, 2048], U32, name="w1q", align_bytes=64)
-        w1s = const.tile([P, 2048], U8, name="w1s", align_bytes=64)
-        w1g = [const.tile([P, 512, 4], BF16, name="w1g%d" % unit, align_bytes=64) for unit in range(4)]
-        w2q = const.tile([P, 1024], U32, name="w2q", align_bytes=64)
-        w2s = const.tile([P, 1024], U8, name="w2s", align_bytes=64)
-        w2g = [const.tile([P, 512, 4], BF16, name="w2g%d" % hf, align_bytes=64) for hf in range(2)]
-
-        def regroup1(engine, unit):
-            regroup(engine, w1g[unit][:], raw1[:, 2 * unit : 2 * unit + 2, :].rearrange("p u (e c) -> p (u e) c", e=2))
-
-        def quant1(unit):
-            nc.vector.quantize_mx(
-                out=w1q[:, 512 * unit : 512 * unit + 512].bitcast(FP8X4),
-                scales=w1s[:, 512 * unit : 512 * unit + 512],
-                in_=w1g[unit][:].rearrange("p c t -> p (c t)"),
+        w2_pool = ctx.enter_context(tc.tile_pool(name="w2", bufs=1))
+        with tc.tile_pool(name="head", bufs=1) as head:
+            x_sb = head.tile([P, 2048], BF16, name="x_sb")
+            nc.sync.dma_start(
+                out=x_sb[:].rearrange("p (h d) -> p h d", h=2),
+                in_=x_attn.flatten_outer_dims().rearrange("(h p) d -> p h d", p=P),
             )
+            raw1 = head.tile([P, 8, 1024], BF16, name="raw1")
+            w1_view = cw1.rearrange("(s q e) c -> q s (e c)", s=8, q=P, e=2)
+            for unit in range(4):
+                nc.sync.dma_start(out=raw1[:, 2 * unit : 2 * unit + 2, :], in_=w1_view[:, 2 * unit : 2 * unit + 2, :])
+            raw2 = w2_pool.tile([P, 4, 1024], BF16, name="raw2")
+            w2_view = cw2.rearrange("(t p) n -> p t n", p=P)
+            for hf in range(2):
+                nc.sync.dma_start(out=raw2[:, :, 512 * hf : 512 * hf + 512], in_=w2_view[:, :, 512 * hf : 512 * hf + 512])
 
-        def quant2(hf):
-            nc.vector.quantize_mx(
-                out=w2q[:, 512 * hf : 512 * hf + 512].bitcast(FP8X4),
-                scales=w2s[:, 512 * hf : 512 * hf + 512],
-                in_=w2g[hf][:].rearrange("p c t -> p (c t)"),
-            )
+            ident_f = const.tile([P, P], F32, name="ident_f")
+            make_identity(nc, ident_f[:])
+            sm = const.tile([P, P], BF16, name="sm")
+            nc.vector.memset(sm[:], 0.0)
+            rows = const.tile([P, 1024], BF16, name="rows")
+            nc.vector.memset(rows[:], 0.0)
+            nc.scalar.dma_start(out=sm[0:8, :], in_=cln_g.rearrange("(c p) -> c p", p=P))
+            nc.scalar.dma_start(out=sm[8:12, :], in_=cb1.rearrange("(t p) -> t p", p=P))
+            nc.scalar.dma_start(out=rows[0:1, :], in_=cln_b.rearrange("(o n) -> o n", o=1))
+            nc.scalar.dma_start(out=rows[32:33, :], in_=cb2.rearrange("(o n) -> o n", o=1))
+            warm = const.tile([P, 2], F32, name="warm")
+            nc.vector.memset(warm[:], 0.0)
+            warm_o = const.tile([P, 2], BF16, name="warm_o")
+            nc.scalar.activation(out=warm_o[:], in_=warm[:], func=ACT.Gelu)
+            ident_b = const.tile([P, P], BF16, name="ident_b")
+            nc.vector.tensor_copy(out=ident_b[:], in_=ident_f[:])
+            pick = const.tile([P, P], BF16, name="pick")
+            nc.vector.memset(pick[:], 0.0)
+            nc.vector.memset(pick[32:33, :], 1.0)
+            deps = const.tile([P, 1], F32, name="deps")
+            nc.vector.tensor_scalar(out=deps[:], in0=warm[:, 0:1], scalar1=1.0, scalar2=D * EPS, op0=ALU.mult, op1=ALU.add)
+            cnt = {}
+            for a, step_k, base in (("H", 1, 17), ("L", -1, 16)):
+                cnt_i = const.tile([P, P], I32, name="cnt_i" + a)
+                nc.gpsimd.iota(cnt_i[:], pattern=[[0, B], [step_k, 16]], base=base, channel_multiplier=0)
+                cnt[a] = const.tile([P, P], BF16, name="cnt" + a)
+                nc.vector.memset(cnt[a][:], 0.0)
+                nc.vector.tensor_scalar(out=cnt[a][0:1, :], in0=cnt_i[0:1, :], scalar1=1.0 / 32.0, scalar2=None, op0=ALU.mult)
 
-        a_pos = const.tile([P, B, 32, 4], F32, name="a_pos")
-        eT = const.tile([P, 256, 4], F32, name="eT")
-        ps1 = {}
+            xw = x_sb[:].bitcast(F32)
+            xg = head.tile([P, 2048], BF16, name="xg", align_bytes=64)
+            xgw = xg[:].bitcast(F32)
+            for g in range(2):
+                xt = psum.tile([P, 2, 2, P], F32, name="xt%d" % g, tag="p%s0" % "ab"[g])
+                for h in range(2):
+                    for u in range(2):
+                        col = 512 * h + 256 * g + 128 * u
+                        nc.tensor.transpose(xt[:, h, u, :], xw[:, col : col + 128], ident_f[:])
+                dst = xgw[:, 512 * g : 512 * g + 512].rearrange("p (h r u) -> p h r u", h=2, u=2)
+                src = xt[:].rearrange("p h u r -> p h r u")
+                if g == 0:
+                    nc.vector.tensor_copy(out=dst, in_=src)
+                else:
+                    nc.scalar.copy(out=dst, in_=src)
+            xq = head.tile([P, 512], U32, name="xq", align_bytes=64)
+            xs = head.tile([P, 512], U8, name="xs", align_bytes=64)
 
-        def first_mm(half):
-            for h in range(2):
-                ps1[(half, h)] = psum.tile([P, 4, P], F32, name="ps1_%d%d" % (half, h), tag="ye"[half] + str(h))
-                for t2 in range(4):
-                    for g in range(2):
-                        wc = 512 * (2 * half + g) + 128 * t2
-                        xc = 256 * g + 128 * h
-                        nc.tensor.matmul_mx(
-                            out=ps1[(half, h)][:, t2, :],
-                            lhsT=w1q[:, wc : wc + 128].bitcast(FP8X4),
-                            lhsT_scale=w1s[:, wc : wc + 128],
-                            rhs=xq[:, xc : xc + 128].bitcast(FP8X4),
-                            rhs_scale=xs[:, xc : xc + 128],
-                            start=(g == 0),
-                            stop=(g == 1),
-                        )
+            def regroup(engine, dst, src):
+                d = dst.rearrange("p (c i) t -> p c t i", i=4)
+                s = src.rearrange("p t (c i) -> p c t i", i=4)
+                if engine == "v":
+                    nc.vector.tensor_copy(out=d, in_=s)
+                else:
+                    nc.scalar.copy(out=d, in_=s)
 
-        regroup1("v", 0)
-        regroup1("s", 1)
-        nc.vector.quantize_mx(out=xq[:].bitcast(FP8X4), scales=xs[:], in_=xg[:])
-        quant1(0)
-        sm_ps = psum.tile([P, P], BF16, name="sm_ps", tag="pa1")
-        nc.tensor.transpose(sm_ps[:], sm[:], ident_b[:])
-        smT = const.tile([P, 12], F32, name="smT")
-        nc.vector.tensor_copy(out=smT[:], in_=sm_ps[:, 0:12])
-        regroup1("v", 2)
-        quant1(1)
-        first_mm(0)
-        regroup1("s", 3)
-        quant1(2)
-        quant1(3)
-        first_mm(1)
+            w1q = head.tile([P, 2048], U32, name="w1q", align_bytes=64)
+            w1s = head.tile([P, 2048], U8, name="w1s", align_bytes=64)
+            w1g = [head.tile([P, 512, 4], BF16, name="w1g%d" % unit, align_bytes=64) for unit in range(4)]
+            w2q = const.tile([P, 1024], U32, name="w2q", align_bytes=64)
+            w2s = const.tile([P, 1024], U8, name="w2s", align_bytes=64)
+            w2g = [w2_pool.tile([P, 512, 4], BF16, name="w2g%d" % hf, align_bytes=64) for hf in range(2)]
+
+            def regroup1(engine, unit):
+                regroup(engine, w1g[unit][:], raw1[:, 2 * unit : 2 * unit + 2, :].rearrange("p u (e c) -> p (u e) c", e=2))
+
+            def quant1(unit):
+                nc.vector.quantize_mx(
+                    out=w1q[:, 512 * unit : 512 * unit + 512].bitcast(FP8X4),
+                    scales=w1s[:, 512 * unit : 512 * unit + 512],
+                    in_=w1g[unit][:].rearrange("p c t -> p (c t)"),
+                )
+
+            def quant2(hf):
+                nc.vector.quantize_mx(
+                    out=w2q[:, 512 * hf : 512 * hf + 512].bitcast(FP8X4),
+                    scales=w2s[:, 512 * hf : 512 * hf + 512],
+                    in_=w2g[hf][:].rearrange("p c t -> p (c t)"),
+                )
+
+            a_pos = const.tile([P, B, 32, 4], F32, name="a_pos")
+            eT = const.tile([P, 256, 4], F32, name="eT")
+            ps1 = {}
+
+            def first_mm(half):
+                for h in range(2):
+                    ps1[(half, h)] = psum.tile([P, 4, P], F32, name="ps1_%d%d" % (half, h), tag="ye"[half] + str(h))
+                    for t2 in range(4):
+                        for g in range(2):
+                            wc = 512 * (2 * half + g) + 128 * t2
+                            xc = 256 * g + 128 * h
+                            nc.tensor.matmul_mx(
+                                out=ps1[(half, h)][:, t2, :],
+                                lhsT=w1q[:, wc : wc + 128].bitcast(FP8X4),
+                                lhsT_scale=w1s[:, wc : wc + 128],
+                                rhs=xq[:, xc : xc + 128].bitcast(FP8X4),
+                                rhs_scale=xs[:, xc : xc + 128],
+                                start=(g == 0),
+                                stop=(g == 1),
+                            )
+
+            regroup1("v", 0)
+            regroup1("s", 1)
+            nc.vector.quantize_mx(out=xq[:].bitcast(FP8X4), scales=xs[:], in_=xg[:])
+            quant1(0)
+            sm_ps = psum.tile([P, P], BF16, name="sm_ps", tag="pa1")
+            nc.tensor.transpose(sm_ps[:], sm[:], ident_b[:])
+            smT = const.tile([P, 12], F32, name="smT")
+            nc.vector.tensor_copy(out=smT[:], in_=sm_ps[:, 0:12])
+            regroup1("v", 2)
+            quant1(1)
+            first_mm(0)
+            regroup1("s", 3)
+            regroup("s", w2g[0][:], raw2[:, :, 0:512])
+            quant1(2)
+            quant1(3)
+            first_mm(1)
+        y_pool = ctx.enter_context(tc.tile_pool(name="y", bufs=8))
+        z_pool = ctx.enter_context(tc.tile_pool(name="z", bufs=8))
         bias = smT[:, 8:12].unsqueeze(1).unsqueeze(1).to_broadcast([P, 4, 16, 4])
         for lo in range(2):
             for h in range(2):
@@ -208,13 +205,12 @@ def tile_causalexpert_pa_t_kernel(tc, x_attn, cw1, cb1, cw2, cb2, cln_g, cln_b, 
         nm = const.tile([P, N_TILES], F32, name="nm")
         ssq = const.tile([P, N_TILES], F32, name="ssq")
         wv = const.tile([P, N_TILES], F32, name="wv")
-        nmw = const.tile([P, N_TILES], F32, name="nmw")
         hq = const.tile([P, P * N_TILES], U32, name="hq", align_bytes=64)
         hs = const.tile([P, P * N_TILES], U8, name="hs", align_bytes=64)
+        h2 = const.tile([P, 512 * N_TILES], BF16, name="h2", align_bytes=64)
 
         acc = {}
         hp_t = {}
-        h2_t = {}
         yps_t = {}
         y_t = {}
         z_t = {}
@@ -244,14 +240,13 @@ def tile_causalexpert_pa_t_kernel(tc, x_attn, cw1, cb1, cw2, cb2, cln_g, cln_b, 
                             )
 
         def stage_gelu(g):
-            n = groups[g][1]
-            h2_t[g] = h2_pool.tile([P, 2048], BF16, name="h2", align_bytes=64)
-            nc.scalar.activation(out=h2_t[g][:, 0 : 512 * n], in_=hp_t[g][:, 0 : 512 * n], func=ACT.Gelu)
-
-        def stage_quant(g):
             t0, n = groups[g]
-            sl = slice(P * t0, P * (t0 + n))
-            nc.vector.quantize_mx(out=hq[:, sl].bitcast(FP8X4), scales=hs[:, sl], in_=h2_t[g][:, 0 : 512 * n])
+            nc.scalar.activation(out=h2[:, 512 * t0 : 512 * (t0 + n)], in_=hp_t[g][:, 0 : 512 * n], func=ACT.Gelu)
+
+        def stage_quant(k):
+            first, count = QUANTS[k]
+            sl = slice(P * first, P * (first + count))
+            nc.vector.quantize_mx(out=hq[:, sl].bitcast(FP8X4), scales=hs[:, sl], in_=h2[:, 512 * first : 512 * (first + count)])
 
         def stage_mm(t):
             for hf in range(2):
@@ -287,8 +282,9 @@ def tile_causalexpert_pa_t_kernel(tc, x_attn, cw1, cb1, cw2, cb2, cln_g, cln_b, 
             junk = junk_pool.tile([P, 1024], BF16, name="junk")
             nc.scalar.activation(out=junk[:], in_=y_t[t][:], func=ACT.Square, bias=nm[:, t : t + 1], scale=1.0, accum_out=ssq[:, t : t + 1])
 
-        def stage_weight(t):
-            nc.scalar.activation(out=wv[:, t : t + 1], in_=ssq[:, t : t + 1], func=ACT.Abs_reciprocal_sqrt, bias=deps[:], scale=1.0)
+        def stage_weight(t, n):
+            sl = slice(t, t + n)
+            nc.scalar.activation(out=wv[:, sl], in_=ssq[:, sl], func=ACT.Abs_reciprocal_sqrt, bias=deps[:], scale=1.0)
 
         def stage_z(t):
             z_t[t] = z_pool.tile([P, 1024], F32, name="z")
@@ -296,14 +292,10 @@ def tile_causalexpert_pa_t_kernel(tc, x_attn, cw1, cb1, cw2, cb2, cln_g, cln_b, 
             wd = 1024 // len(eng)
             for k in range(len(eng)):
                 sl = slice(wd * k, wd * k + wd)
-                if eng[k] == "a":
-                    nc.scalar.activation(out=nmw[:, t : t + 1], in_=nm[:, t : t + 1], func=ACT.Copy, scale=wv[:, t : t + 1])
-                    nc.scalar.activation(out=z_t[t][:, sl], in_=y_t[t][:, sl], func=ACT.Identity, bias=nmw[:, t : t + 1], scale=wv[:, t : t + 1])
-                else:
-                    engine = nc.gpsimd if eng[k] == "g" else nc.vector
-                    engine.tensor_scalar(
-                        out=z_t[t][:, sl], in0=y_t[t][:, sl], scalar1=nm[:, t : t + 1], scalar2=wv[:, t : t + 1], op0=ALU.add, op1=ALU.mult
-                    )
+                engine = nc.gpsimd if eng[k] == "g" else nc.vector
+                engine.tensor_scalar(
+                    out=z_t[t][:, sl], in0=y_t[t][:, sl], scalar1=nm[:, t : t + 1], scalar2=wv[:, t : t + 1], op0=ALU.add, op1=ALU.mult
+                )
 
         def stage_sum(t):
             w = tiles[t][0]
@@ -321,7 +313,7 @@ def tile_causalexpert_pa_t_kernel(tc, x_attn, cw1, cb1, cw2, cb2, cln_g, cln_b, 
                         acc[key] = psum.tile([P, 4, B, 16], F32, name="acc2_%d" % (c // 4), tag="pa%d" % (c // 4))
                     dst = acc[key][:, c % 4, :, :]
                     first = t == N_PHASE1 and c % 4 == 0
-                    last = t == N_TILES - 1 and c % 4 == 3
+                    last = t == N_TILES - 2 and c % 4 == 3
                 nc.tensor.matmul(dst, lhsT=z_t[t][:, 128 * c : 128 * c + 128], rhs=ident3, is_transpose=True, start=first, stop=last)
 
         oT = {}
@@ -330,17 +322,17 @@ def tile_causalexpert_pa_t_kernel(tc, x_attn, cw1, cb1, cw2, cb2, cln_g, cln_b, 
         back = {}
 
         def stage_mid():
-            for bank in range(2):
+            for bank in (0, 2):
                 gain = smT[:, 2 * bank : 2 * bank + 2].unsqueeze(2).unsqueeze(3).to_broadcast([P, 2, B, 16])
                 for a, p0 in (("L", 16), ("H1", 0)):
                     nc.vector.tensor_tensor(
                         out=oT[a][:, 2 * bank : 2 * bank + 2, :, :], in0=acc[(1, bank)][:, :, :, p0 : p0 + 16], in1=gain, op=ALU.mult
                     )
-            for a, p0 in (("L", 16), ("H1", 0)):
-                for c in range(4, 8):
-                    nc.scalar.activation(
-                        out=oT[a][:, c, :, :], in_=acc[(1, c // 2)][:, c % 2, :, p0 : p0 + 16], func=ACT.Copy, scale=smT[:, c : c + 1]
-                    )
+                for c in (2 * bank + 2, 2 * bank + 3):
+                    for a, p0 in (("L", 16), ("H1", 0)):
+                        nc.scalar.activation(
+                            out=oT[a][:, c, :, :], in_=acc[(1, c // 2)][:, c % 2, :, p0 : p0 + 16], func=ACT.Copy, scale=smT[:, c : c + 1]
+                        )
 
         def back_open(a):
             for hb in range(2):
@@ -370,14 +362,19 @@ def tile_causalexpert_pa_t_kernel(tc, x_attn, cw1, cb1, cw2, cb2, cln_g, cln_b, 
 
         def stage_store(a):
             osb = const.tile([P, 1024], F32, name="osb" + a)
-            nc.vector.tensor_copy(out=osb[:, 0:512], in_=back[(a, 0)][:])
-            nc.scalar.copy(out=osb[:, 512:1024], in_=back[(a, 1)][:])
-            if a == "H":
-                for b in range(B):
-                    nc.sync.dma_start(out=out[b, 16:32, :], in_=osb[16 * b : 16 * b + 16, :])
-            else:
+            if a == "L":
+                nc.vector.tensor_copy(out=osb[:, 0:512], in_=back[(a, 0)][:])
+                nc.scalar.copy(out=osb[:, 512:1024], in_=back[(a, 1)][:])
                 for k in range(16):
                     nc.sync.dma_start(out=out[:, 15 - k, :], in_=osb[k : P : 16, :])
+                return
+            for hb in range(2):
+                cols = slice(512 * hb, 512 * hb + 512)
+                nc.vector.scalar_tensor_tensor(
+                    out=osb[:, cols], in0=yg[:, cols], scalar=wv[:, N_TILES - 1 :], in1=back[(a, hb)][:], op0=ALU.mult, op1=ALU.add
+                )
+            for b in range(B):
+                nc.sync.dma_start(out=out[b, 16:32, :], in_=osb[16 * b : 16 * b + 16, :])
 
         for h in range(2):
             nc.scalar.copy(out=eT[:, 128 * h : 128 * h + 128, :], in_=ps1[(1, h)][:].rearrange("p t r -> p r t"))
@@ -388,51 +385,69 @@ def tile_causalexpert_pa_t_kernel(tc, x_attn, cw1, cb1, cw2, cb2, cln_g, cln_b, 
         cb_ps = []
         for hf in range(2):
             cb_ps.append(psum.tile([P, 512], F32, name="cb_ps%d" % hf, tag="p%s1" % "ab"[hf]))
-            nc.tensor.matmul(cb_ps[hf][:], lhsT=pick0[:], rhs=rows[:, 512 * hf : 512 * hf + 512], start=True, stop=True)
+            nc.tensor.matmul(cb_ps[hf][:], lhsT=pick[:], rhs=rows[:, 512 * hf : 512 * hf + 512], start=True, stop=True)
         for g in range(2, n_groups):
             stage_add(g)
-            if g == 3:
+            if g == 4:
+                quant2(0)
+            if g == 5:
+                regroup("v", w2g[1][:], raw2[:, :, 512:1024])
+            if g == 6:
+                quant2(1)
+            if g == 5:
                 for hf in range(2):
                     nc.scalar.copy(out=cb2_bc[:, 512 * hf : 512 * hf + 512], in_=cb_ps[hf][:])
-            if g in (4, 6):
-                hf = (g - 4) // 2
-                regroup("v", w2g[hf][:], raw2[:, :, 512 * hf : 512 * hf + 512])
-            if g in (5, 7):
-                quant2((g - 5) // 2)
             stage_gelu(g - 1)
-            stage_quant(g - 2)
         stage_gelu(n_groups - 1)
+        nc.scalar.activation(out=warm_o[:], in_=warm[:], func=ACT.Abs_reciprocal_sqrt, bias=deps[:], scale=1.0)
+        for k in range(2):
+            stage_quant(k)
+        g_bc = const.tile([P, 1024], BF16, name="g_bc")
+        nc.vector.memset(g_bc[:, 0:2], 0.0)
+        nc.sync.dma_start(out=g_bc[:], in_=cln_g.partition_broadcast(P))
         stage_mm(0)
         stage_mm(1)
 
-        for step in range(0, N_TILES + LAG_SUM2):
-            if step < N_TILES:
-                stage_bias(step)
-                stage_nm(step)
-            if 0 <= step - 1 < N_TILES:
-                stage_weight(step - 1)
-            if step < N_TILES:
-                stage_square(step)
-            if step in (1, 2):
-                stage_quant(n_groups - 3 + step)
-            if step + 2 < N_TILES:
+        last = N_TILES - 1
+        yg = const.tile([P, 1024], F32, name="yg")
+        weights_at = {}
+        for t in range(0, last - 2, 2):
+            weights_at.setdefault(t + 3, []).append((t, 2))
+        sums_at = {t + 5: (t, t + 1) for t in range(0, 16, 2)}
+        sums_at.update({21: (16,), 23: (17, 18), 24: (19, 20), 26: (21, 22), 28: (23, 24), 30: (25, 26), 32: (27, 28)})
+        for step in range(last + 1):
+            stage_bias(step)
+            stage_nm(step)
+            for t, n in weights_at.get(step, []):
+                stage_weight(t, n)
+            if step >= 1:
+                stage_square(step - 1)
+            if step >= last - 1:
+                stage_weight(step - 1, 1)
+            if step in (1, 3, 5):
+                stage_quant(2 + step // 2)
+            if step + 2 <= last:
                 stage_mm(step + 2)
-            if 0 <= step - LAG_Z < N_TILES:
-                stage_z(step - LAG_Z)
-            if step - LAG_SUM == N_PHASE1:
+            if step >= 3:
+                stage_z(step - 3)
+            if step == 22:
                 stage_mid()
-            if 0 <= step - LAG_SUM < N_PHASE1:
-                stage_sum(step - LAG_SUM)
-            if N_PHASE1 <= step - LAG_SUM2 < N_TILES:
-                stage_sum(step - LAG_SUM2)
-            if step - LAG_SUM2 == N_PHASE1:
+            for t in sums_at.get(step, ()):
+                stage_sum(t)
+            if step == 26:
                 back_open("L")
                 back_add("L", oT["L"], True)
-            if step - LAG_SUM2 == N_PHASE1 + 2:
+            if step == 28:
                 stage_store("L")
-            if step - LAG_SUM2 == N_PHASE1 + 4:
-                back_open("H")
-                back_add("H", oT["H1"], False)
+        stage_square(last)
+        stage_weight(last, 1)
+        for t in (last - 2, last - 1):
+            stage_z(t)
+        nc.vector.scalar_tensor_tensor(out=yg[:], in0=y_t[last][:], scalar=nm[:, last:], in1=g_bc[:], op0=ALU.add, op1=ALU.mult)
+        back_open("H")
+        back_add("H", oT["H1"], False)
+        for t in (last - 3, last - 2, last - 1):
+            stage_sum(t)
         stage_last()
         back_add("H", oT["H2"], True)
         stage_store("H")

@@ -21,7 +21,7 @@ N_PHASE1 = 17
 N_TILES = 33
 GROUPS = [1, 2, 2] + [4] * 7
 QUANTS = [(0, 1), (1, 8), (9, 8), (17, 8), (25, 8)]
-G_ADDS = (4, 7, 8, 12, 15, 16, 20, 23, 24, 28)
+G_ADDS = (4, 8, 12, 16, 20, 24)
 
 
 def z_engines(t):
@@ -389,16 +389,13 @@ def tile_causalexpert_pa_t_kernel(tc, x_attn, cw1, cb1, cw2, cb2, cln_g, cln_b, 
         for g in range(2, n_groups):
             stage_add(g)
             if g == 4:
-                quant2(0)
-            if g == 5:
-                regroup("v", w2g[1][:], raw2[:, :, 512:1024])
-            if g == 6:
-                quant2(1)
-            if g == 5:
                 for hf in range(2):
                     nc.scalar.copy(out=cb2_bc[:, 512 * hf : 512 * hf + 512], in_=cb_ps[hf][:])
             stage_gelu(g - 1)
         stage_gelu(n_groups - 1)
+        quant2(0)
+        regroup("v", w2g[1][:], raw2[:, :, 512:1024])
+        quant2(1)
         nc.scalar.activation(out=warm_o[:], in_=warm[:], func=ACT.Abs_reciprocal_sqrt, bias=deps[:], scale=1.0)
         for k in range(2):
             stage_quant(k)
@@ -410,10 +407,11 @@ def tile_causalexpert_pa_t_kernel(tc, x_attn, cw1, cb1, cw2, cb2, cln_g, cln_b, 
 
         last = N_TILES - 1
         yg = const.tile([P, 1024], F32, name="yg")
-        weights_at = {}
-        for t in range(0, last - 2, 2):
+        weights_at = {2: [(0, 1)], 3: [(1, 1)]}
+        for t in range(2, last - 2, 2):
             weights_at.setdefault(t + 3, []).append((t, 2))
         sums_at = {t + 5: (t, t + 1) for t in range(0, 16, 2)}
+        sums_at.update({4: (0,), 5: (1,)})
         sums_at.update({21: (16,), 23: (17, 18), 24: (19, 20), 26: (21, 22), 28: (23, 24), 30: (25, 26), 32: (27, 28)})
         for step in range(last + 1):
             stage_bias(step)
@@ -439,13 +437,14 @@ def tile_causalexpert_pa_t_kernel(tc, x_attn, cw1, cb1, cw2, cb2, cln_g, cln_b, 
                 back_add("L", oT["L"], True)
             if step == 28:
                 stage_store("L")
+            if step == 30:
+                back_open("H")
+                back_add("H", oT["H1"], False)
         stage_square(last)
         stage_weight(last, 1)
-        for t in (last - 2, last - 1):
-            stage_z(t)
+        stage_z(last - 2)
         nc.vector.scalar_tensor_tensor(out=yg[:], in0=y_t[last][:], scalar=nm[:, last:], in1=g_bc[:], op0=ALU.add, op1=ALU.mult)
-        back_open("H")
-        back_add("H", oT["H1"], False)
+        stage_z(last - 1)
         for t in (last - 3, last - 2, last - 1):
             stage_sum(t)
         stage_last()

@@ -21,7 +21,7 @@ N_PHASE1 = 17
 N_TILES = 33
 GROUPS = [1, 2, 2] + [4] * 7
 QUANTS = [(0, 1), (1, 8), (9, 8), (17, 8), (25, 8)]
-G_ADDS = (4, 8, 12, 16, 20, 24)
+G_ADDS = (8, 12, 16, 20, 24)
 
 
 def z_engines(t):
@@ -114,10 +114,7 @@ def tile_causalexpert_pa_t_kernel(tc, x_attn, cw1, cb1, cw2, cb2, cln_g, cln_b, 
                         nc.tensor.transpose(xt[:, h, u, :], xw[:, col : col + 128], ident_f[:])
                 dst = xgw[:, 512 * g : 512 * g + 512].rearrange("p (h r u) -> p h r u", h=2, u=2)
                 src = xt[:].rearrange("p h u r -> p h r u")
-                if g == 0:
-                    nc.vector.tensor_copy(out=dst, in_=src)
-                else:
-                    nc.scalar.copy(out=dst, in_=src)
+                nc.scalar.copy(out=dst, in_=src)
             xq = head.tile([P, 512], U32, name="xq", align_bytes=64)
             xs = head.tile([P, 512], U8, name="xs", align_bytes=64)
 
@@ -136,14 +133,27 @@ def tile_causalexpert_pa_t_kernel(tc, x_attn, cw1, cb1, cw2, cb2, cln_g, cln_b, 
             w2s = const.tile([P, 1024], U8, name="w2s", align_bytes=64)
             w2g = [w2_pool.tile([P, 512, 4], BF16, name="w2g%d" % hf, align_bytes=64) for hf in range(2)]
 
-            def regroup1(engine, unit):
-                regroup(engine, w1g[unit][:], raw1[:, 2 * unit : 2 * unit + 2, :].rearrange("p u (e c) -> p (u e) c", e=2))
+            def regroup2(hf):
+                for k in range(4):
+                    col = 512 * hf + 128 * k
+                    nc.gpsimd.tensor_scalar(
+                        out=w2g[hf][:, 128 * k : 128 * k + 128, :].rearrange("p (c i) t -> p c t i", i=4),
+                        in0=raw2[:, :, col : col + 128].rearrange("p t (c i) -> p c t i", i=4),
+                        scalar1=1.0,
+                        scalar2=0.0,
+                        op0=ALU.mult,
+                        op1=ALU.add,
+                    )
 
-            def quant1(unit):
+            def regroup1(engine, unit, c0=0, c1=512):
+                src = raw1[:, 2 * unit : 2 * unit + 2, :].rearrange("p u (e c) -> p (u e) c", e=2)
+                regroup(engine, w1g[unit][:, c0:c1, :], src[:, :, c0:c1])
+
+            def quant1(unit, c0=0, c1=512):
                 nc.vector.quantize_mx(
-                    out=w1q[:, 512 * unit : 512 * unit + 512].bitcast(FP8X4),
-                    scales=w1s[:, 512 * unit : 512 * unit + 512],
-                    in_=w1g[unit][:].rearrange("p c t -> p (c t)"),
+                    out=w1q[:, 512 * unit + c0 : 512 * unit + c1].bitcast(FP8X4),
+                    scales=w1s[:, 512 * unit + c0 : 512 * unit + c1],
+                    in_=w1g[unit][:, c0:c1, :].rearrange("p c t -> p (c t)"),
                 )
 
             def quant2(hf):
@@ -157,10 +167,11 @@ def tile_causalexpert_pa_t_kernel(tc, x_attn, cw1, cb1, cw2, cb2, cln_g, cln_b, 
             eT = const.tile([P, 256, 4], F32, name="eT")
             ps1 = {}
 
-            def first_mm(half):
-                for h in range(2):
-                    ps1[(half, h)] = psum.tile([P, 4, P], F32, name="ps1_%d%d" % (half, h), tag="ye"[half] + str(h))
-                    for t2 in range(4):
+            def first_mm(half, chunks):
+                for t2 in chunks:
+                    for h in range(2):
+                        if t2 == 0:
+                            ps1[(half, h)] = psum.tile([P, 4, P], F32, name="ps1_%d%d" % (half, h), tag="ye"[half] + str(h))
                         for g in range(2):
                             wc = 512 * (2 * half + g) + 128 * t2
                             xc = 256 * g + 128 * h
@@ -182,14 +193,23 @@ def tile_causalexpert_pa_t_kernel(tc, x_attn, cw1, cb1, cw2, cb2, cln_g, cln_b, 
             nc.tensor.transpose(sm_ps[:], sm[:], ident_b[:])
             smT = const.tile([P, 12], F32, name="smT")
             nc.vector.tensor_copy(out=smT[:], in_=sm_ps[:, 0:12])
+            cb2_bc = const.tile([P, 1024], F32, name="cb2_bc")
+            cb_ps = []
+            for hf in range(2):
+                cb_ps.append(psum.tile([P, 512], F32, name="cb_ps%d" % hf, tag="p%s1" % "ab"[hf]))
+                nc.tensor.matmul(cb_ps[hf][:], lhsT=pick[:], rhs=rows[:, 512 * hf : 512 * hf + 512], start=True, stop=True)
             regroup1("v", 2)
             quant1(1)
-            first_mm(0)
-            regroup1("s", 3)
-            regroup("s", w2g[0][:], raw2[:, :, 0:512])
+            first_mm(0, range(4))
             quant1(2)
-            quant1(3)
-            first_mm(1)
+            for c0 in (0, 256):
+                regroup1("s", 3, c0, c0 + 256)
+                quant1(3, c0, c0 + 256)
+                first_mm(1, range(c0 // 128, c0 // 128 + 2))
+            for hf in range(2):
+                nc.scalar.copy(out=cb2_bc[:, 512 * hf : 512 * hf + 512], in_=cb_ps[hf][:])
+            nc.vector.memset(w2g[0][:, 0:1, :], 0.0)
+            regroup2(0)
         y_pool = ctx.enter_context(tc.tile_pool(name="y", bufs=8))
         z_pool = ctx.enter_context(tc.tile_pool(name="z", bufs=8))
         bias = smT[:, 8:12].unsqueeze(1).unsqueeze(1).to_broadcast([P, 4, 16, 4])
@@ -381,20 +401,13 @@ def tile_causalexpert_pa_t_kernel(tc, x_attn, cw1, cb1, cw2, cb2, cln_g, cln_b, 
         stage_add(0)
         stage_add(1)
         stage_gelu(0)
-        cb2_bc = const.tile([P, 1024], F32, name="cb2_bc")
-        cb_ps = []
-        for hf in range(2):
-            cb_ps.append(psum.tile([P, 512], F32, name="cb_ps%d" % hf, tag="p%s1" % "ab"[hf]))
-            nc.tensor.matmul(cb_ps[hf][:], lhsT=pick[:], rhs=rows[:, 512 * hf : 512 * hf + 512], start=True, stop=True)
         for g in range(2, n_groups):
             stage_add(g)
-            if g == 4:
-                for hf in range(2):
-                    nc.scalar.copy(out=cb2_bc[:, 512 * hf : 512 * hf + 512], in_=cb_ps[hf][:])
+            if g == 8:
+                regroup2(1)
             stage_gelu(g - 1)
         stage_gelu(n_groups - 1)
         quant2(0)
-        regroup("v", w2g[1][:], raw2[:, :, 512:1024])
         quant2(1)
         nc.scalar.activation(out=warm_o[:], in_=warm[:], func=ACT.Abs_reciprocal_sqrt, bias=deps[:], scale=1.0)
         for k in range(2):

@@ -65,10 +65,10 @@ def tile_causalexpert_pa_t_kernel(tc, x_attn, cw1, cb1, cw2, cb2, cln_g, cln_b, 
                 out=x_sb[:].rearrange("p (h d) -> p h d", h=2),
                 in_=x_attn.flatten_outer_dims().rearrange("(h p) d -> p h d", p=P),
             )
-            raw1 = head.tile([P, 8, 1024], BF16, name="raw1")
-            w1_view = cw1.rearrange("(s q e) c -> q s (e c)", s=8, q=P, e=2)
+            raw1 = head.tile([P, 4, 2048], BF16, name="raw1")
+            w1_view = cw1.rearrange("(g p j) c -> p g (j c)", g=4, p=P, j=4)
             for unit in range(4):
-                nc.sync.dma_start(out=raw1[:, 2 * unit : 2 * unit + 2, :], in_=w1_view[:, 2 * unit : 2 * unit + 2, :])
+                nc.sync.dma_start(out=raw1[:, unit, :], in_=w1_view[:, unit, :])
             raw2 = w2_pool.tile([P, 4, 1024], BF16, name="raw2")
             w2_view = cw2.rearrange("(t p) n -> p t n", p=P)
             for hf in range(2):
@@ -110,8 +110,8 @@ def tile_causalexpert_pa_t_kernel(tc, x_attn, cw1, cb1, cw2, cb2, cln_g, cln_b, 
                 xt = psum.tile([P, 2, 2, P], F32, name="xt%d" % g, tag="p%s0" % "ab"[g])
                 for h in range(2):
                     for u in range(2):
-                        col = 512 * h + 256 * g + 128 * u
-                        nc.tensor.transpose(xt[:, h, u, :], xw[:, col : col + 128], ident_f[:])
+                        col = 512 * h + 256 * g
+                        nc.tensor.transpose(xt[:, h, u, :], xw[:, col + u : col + 256 : 2], ident_f[:])
                 dst = xgw[:, 512 * g : 512 * g + 512].rearrange("p (h r u) -> p h r u", h=2, u=2)
                 src = xt[:].rearrange("p h u r -> p h r u")
                 nc.scalar.copy(out=dst, in_=src)
@@ -146,7 +146,7 @@ def tile_causalexpert_pa_t_kernel(tc, x_attn, cw1, cb1, cw2, cb2, cln_g, cln_b, 
                     )
 
             def regroup1(engine, unit, c0=0, c1=512):
-                src = raw1[:, 2 * unit : 2 * unit + 2, :].rearrange("p u (e c) -> p (u e) c", e=2)
+                src = raw1[:, unit, :].rearrange("p (j c) -> p j c", j=4)
                 regroup(engine, w1g[unit][:, c0:c1, :], src[:, :, c0:c1])
 
             def quant1(unit, c0=0, c1=512):

@@ -17,7 +17,6 @@ B, L, D, C = 8, 32, 1024, 512
 EPS = 1e-5
 FLOPS = 2 * (B * L) * (2 * D) * C + 2 * (B * L * (L + 1) // 2) * C * D
 
-N_PHASE1 = 17
 N_TILES = 33
 GROUPS = [1, 2, 2] + [4] * 7
 QUANTS = [(0, 1), (1, 8), (9, 8), (17, 8), (25, 8)]
@@ -96,9 +95,9 @@ def tile_causalexpert_pa_t_kernel(tc, x_attn, cw1, cb1, cw2, cb2, cln_g, cln_b, 
             deps = const.tile([P, 1], F32, name="deps")
             nc.vector.tensor_scalar(out=deps[:], in0=warm[:, 0:1], scalar1=1.0, scalar2=D * EPS, op0=ALU.mult, op1=ALU.add)
             cnt = {}
-            for a, step_k, base in (("H", 1, 17), ("L", -1, 16)):
+            for a, base in (("H", 17), ("L", 1)):
                 cnt_i = const.tile([P, P], I32, name="cnt_i" + a)
-                nc.gpsimd.iota(cnt_i[:], pattern=[[0, B], [step_k, 16]], base=base, channel_multiplier=0)
+                nc.gpsimd.iota(cnt_i[:], pattern=[[0, B], [1, 16]], base=base, channel_multiplier=0)
                 cnt[a] = const.tile([P, P], BF16, name="cnt" + a)
                 nc.vector.memset(cnt[a][:], 0.0)
                 nc.vector.tensor_scalar(out=cnt[a][0:1, :], in0=cnt_i[0:1, :], scalar1=1.0 / 32.0, scalar2=None, op0=ALU.mult)
@@ -320,81 +319,67 @@ def tile_causalexpert_pa_t_kernel(tc, x_attn, cw1, cb1, cw2, cb2, cln_g, cln_b, 
         def stage_sum(t):
             w = tiles[t][0]
             for c in range(8):
-                if t < N_PHASE1:
-                    key = (1, c // 2)
-                    if key not in acc:
-                        acc[key] = psum.tile([P, 2, B, 32], F32, name="acc1_%d" % (c // 2), tag="p%s%d" % ("ab"[c // 4], (c // 2) % 2))
-                    dst = acc[key][:, c % 2, :, w : w + 16]
-                    first = t == 0 and c % 2 == 0
-                    last = t == N_PHASE1 - 1 and c % 2 == 1
-                else:
-                    key = (2, c // 4)
-                    if key not in acc:
-                        acc[key] = psum.tile([P, 4, B, 16], F32, name="acc2_%d" % (c // 4), tag="pa%d" % (c // 4))
-                    dst = acc[key][:, c % 4, :, :]
-                    first = t == N_PHASE1 and c % 4 == 0
-                    last = t == N_TILES - 2 and c % 4 == 3
-                nc.tensor.matmul(dst, lhsT=z_t[t][:, 128 * c : 128 * c + 128], rhs=ident3, is_transpose=True, start=first, stop=last)
+                key = c // 2
+                if key not in acc:
+                    acc[key] = psum.tile([P, 2, B, 32], F32, name="acc%d" % key, tag="p%s%d" % ("ab"[c // 4], key % 2))
+                nc.tensor.matmul(
+                    acc[key][:, c % 2, :, w : w + 16],
+                    lhsT=z_t[t][:, 128 * c : 128 * c + 128],
+                    rhs=ident3,
+                    is_transpose=True,
+                    start=(t == 0 and c % 2 == 0),
+                    stop=(t == N_TILES - 2 and c % 2 == 1),
+                )
 
-        oT = {}
-        for a in ("L", "H1", "H2"):
-            oT[a] = const.tile([P, 8, B, 16], F32, name="oT" + a)
+        oT = const.tile([P, 2, 8, B, 16], F32, name="oT")
         back = {}
 
-        def stage_mid():
-            for bank in (0, 2):
-                gain = smT[:, 2 * bank : 2 * bank + 2].unsqueeze(2).unsqueeze(3).to_broadcast([P, 2, B, 16])
-                for a, p0 in (("L", 16), ("H1", 0)):
+        def stage_empty():
+            for half in range(2):
+                for key in range(2):
+                    gain = smT[:, 2 * key : 2 * key + 2].unsqueeze(2).unsqueeze(3).to_broadcast([P, 2, B, 16])
+                    src = acc[key][:, :, :, 16 * half : 16 * half + 16]
                     nc.vector.tensor_tensor(
-                        out=oT[a][:, 2 * bank : 2 * bank + 2, :, :], in0=acc[(1, bank)][:, :, :, p0 : p0 + 16], in1=gain, op=ALU.mult
+                        out=oT[:, half, 2 * key : 2 * key + 2, :, :], in0=src[:, :, :, ::-1] if half else src, in1=gain, op=ALU.mult
                     )
-                for c in (2 * bank + 2, 2 * bank + 3):
-                    for a, p0 in (("L", 16), ("H1", 0)):
-                        nc.scalar.activation(
-                            out=oT[a][:, c, :, :], in_=acc[(1, c // 2)][:, c % 2, :, p0 : p0 + 16], func=ACT.Copy, scale=smT[:, c : c + 1]
-                        )
+                for c in range(4, 8):
+                    src = acc[c // 2][:, c % 2, :, 16 * half : 16 * half + 16]
+                    nc.scalar.activation(
+                        out=oT[:, half, c, :, :], in_=src[:, :, ::-1] if half else src, func=ACT.Copy, scale=smT[:, c : c + 1]
+                    )
 
         def back_open(a):
             for hb in range(2):
-                back[(a, hb)] = psum.tile([P, 512], F32, name="back%s%d" % (a, hb), tag="pb%d" % hb)
+                back[(a, hb)] = psum.tile([P, 512], F32, name="back%s%d" % (a, hb), tag=("e" if a == "H" else "y") + str(hb))
                 nc.tensor.matmul(back[(a, hb)][:], lhsT=cnt[a][:], rhs=rows[:, 512 * hb : 512 * hb + 512], start=True, stop=False)
 
-        def back_add(a, src, closes):
-            flat = src[:].rearrange("p c b s -> p c (b s)")
+        def back_add(a):
             for hb in range(2):
                 for c in range(4):
                     nc.tensor.matmul(
                         back[(a, hb)][:, 128 * c : 128 * c + 128],
-                        lhsT=flat[:, 4 * hb + c, :],
+                        lhsT=oT[:, "HL".index(a), 4 * hb + c, :, :].rearrange("p b s -> p (b s)"),
                         rhs=ident_f[:],
                         is_transpose=True,
                         start=False,
-                        stop=(closes and c == 3),
+                        stop=(c == 3),
                     )
-
-        def stage_last():
-            gain = smT[:, 0:4].unsqueeze(2).to_broadcast([P, 4, P])
-            nc.vector.tensor_tensor(
-                out=oT["H2"][:, 0:4, :, :].rearrange("p c b s -> p c (b s)"), in0=acc[(2, 0)][:].rearrange("p c b s -> p c (b s)"), in1=gain, op=ALU.mult
-            )
-            for c in range(4, 8):
-                nc.scalar.activation(out=oT["H2"][:, c, :, :], in_=acc[(2, 1)][:, c % 4, :, :], func=ACT.Copy, scale=smT[:, c : c + 1])
 
         def stage_store(a):
             osb = const.tile([P, 1024], F32, name="osb" + a)
-            if a == "L":
-                nc.vector.tensor_copy(out=osb[:, 0:512], in_=back[(a, 0)][:])
-                nc.scalar.copy(out=osb[:, 512:1024], in_=back[(a, 1)][:])
-                for k in range(16):
-                    nc.sync.dma_start(out=out[:, 15 - k, :], in_=osb[k : P : 16, :])
-                return
             for hb in range(2):
                 cols = slice(512 * hb, 512 * hb + 512)
-                nc.vector.scalar_tensor_tensor(
-                    out=osb[:, cols], in0=yg[:, cols], scalar=wv[:, N_TILES - 1 :], in1=back[(a, hb)][:], op0=ALU.mult, op1=ALU.add
-                )
+                if a == "H":
+                    nc.vector.scalar_tensor_tensor(
+                        out=osb[:, cols], in0=yg[:, cols], scalar=wv[:, N_TILES - 1 :], in1=back[(a, hb)][:], op0=ALU.mult, op1=ALU.add
+                    )
+                elif hb == 0:
+                    nc.scalar.copy(out=osb[:, cols], in_=back[(a, hb)][:])
+                else:
+                    nc.vector.tensor_copy(out=osb[:, cols], in_=back[(a, hb)][:])
+            queue, i0 = (nc.sync, 16) if a == "H" else (nc.scalar, 0)
             for b in range(B):
-                nc.sync.dma_start(out=out[b, 16:32, :], in_=osb[16 * b : 16 * b + 16, :])
+                queue.dma_start(out=out[b, i0 : i0 + 16, :], in_=osb[16 * b : 16 * b + 16, :])
 
         for h in range(2):
             nc.scalar.copy(out=eT[:, 128 * h : 128 * h + 128, :], in_=ps1[(1, h)][:].rearrange("p t r -> p r t"))
@@ -425,7 +410,7 @@ def tile_causalexpert_pa_t_kernel(tc, x_attn, cw1, cb1, cw2, cb2, cln_g, cln_b, 
             weights_at.setdefault(t + 3, []).append((t, 2))
         sums_at = {t + 5: (t, t + 1) for t in range(0, 16, 2)}
         sums_at.update({4: (0,), 5: (1,)})
-        sums_at.update({21: (16,), 23: (17, 18), 24: (19, 20), 26: (21, 22), 28: (23, 24), 30: (25, 26), 32: (27, 28)})
+        sums_at.update({t + 5: (t, t + 1) for t in range(16, 28, 2)})
         for step in range(last + 1):
             stage_bias(step)
             stage_nm(step)
@@ -435,31 +420,27 @@ def tile_causalexpert_pa_t_kernel(tc, x_attn, cw1, cb1, cw2, cb2, cln_g, cln_b, 
                 stage_square(step - 1)
             if step >= last - 1:
                 stage_weight(step - 1, 1)
-            if step in (1, 3, 5):
-                stage_quant(2 + step // 2)
+            if step in (0, 1, 2):
+                stage_quant(2 + step)
             if step + 2 <= last:
                 stage_mm(step + 2)
             if step >= 3:
                 stage_z(step - 3)
-            if step == 22:
-                stage_mid()
             for t in sums_at.get(step, ()):
                 stage_sum(t)
-            if step == 26:
-                back_open("L")
-                back_add("L", oT["L"], True)
-            if step == 28:
-                stage_store("L")
-            if step == 30:
-                back_open("H")
-                back_add("H", oT["H1"], False)
         stage_square(last)
         stage_weight(last, 1)
         stage_z(last - 2)
         nc.vector.scalar_tensor_tensor(out=yg[:], in0=y_t[last][:], scalar=nm[:, last:], in1=g_bc[:], op0=ALU.add, op1=ALU.mult)
         stage_z(last - 1)
-        for t in (last - 3, last - 2, last - 1):
+        back_open("H")
+        for t in (last - 4, last - 3):
             stage_sum(t)
-        stage_last()
-        back_add("H", oT["H2"], True)
+        back_open("L")
+        for t in (last - 2, last - 1):
+            stage_sum(t)
+        stage_empty()
+        back_add("H")
+        back_add("L")
         stage_store("H")
+        stage_store("L")

@@ -20,7 +20,7 @@ FLOPS = 2 * (B * L) * (2 * D) * C + 2 * (B * L * (L + 1) // 2) * C * D
 N_TILES = 33
 GROUPS = [1, 2, 2] + [4] * 7
 QUANTS = [(0, 1), (1, 8), (9, 8), (17, 8), (25, 8)]
-G_ADDS = (8, 12, 16, 20, 24)
+G_ADDS = (8, 12, 16, 19, 23)
 
 
 def z_engines(t):
@@ -60,14 +60,16 @@ def tile_causalexpert_pa_t_kernel(tc, x_attn, cw1, cb1, cw2, cb2, cln_g, cln_b, 
         w2_pool = ctx.enter_context(tc.tile_pool(name="w2", bufs=1))
         with tc.tile_pool(name="head", bufs=1) as head:
             x_sb = head.tile([P, 2048], BF16, name="x_sb")
+            raw1 = head.tile([P, 4, 2048], BF16, name="raw1")
+            w1_view = cw1.rearrange("(g p j) c -> p g (j c)", g=4, p=P, j=4)
+            nc.sync.dma_start(out=raw1[:, 0, :], in_=w1_view[:, 0, :])
             nc.sync.dma_start(
                 out=x_sb[:].rearrange("p (h d) -> p h d", h=2),
                 in_=x_attn.flatten_outer_dims().rearrange("(h p) d -> p h d", p=P),
             )
-            raw1 = head.tile([P, 4, 2048], BF16, name="raw1")
-            w1_view = cw1.rearrange("(g p j) c -> p g (j c)", g=4, p=P, j=4)
-            for unit in range(4):
-                nc.sync.dma_start(out=raw1[:, unit, :], in_=w1_view[:, unit, :])
+            nc.sync.dma_start(out=raw1[:, 1, :], in_=w1_view[:, 1, :])
+            nc.sync.dma_start(out=raw1[:, 2, :], in_=w1_view[:, 2, :])
+            nc.sync.dma_start(out=raw1[:, 3, :], in_=w1_view[:, 3, :])
             raw2 = w2_pool.tile([P, 4, 1024], BF16, name="raw2")
             w2_view = cw2.rearrange("(t p) n -> p t n", p=P)
             for hf in range(2):
@@ -163,7 +165,7 @@ def tile_causalexpert_pa_t_kernel(tc, x_attn, cw1, cb1, cw2, cb2, cln_g, cln_b, 
                 )
 
             a_pos = const.tile([P, B, 32, 4], F32, name="a_pos")
-            eT = const.tile([P, 256, 4], F32, name="eT")
+            eT = const.tile([P, 2, B, 4, 4], F32, name="eT")
             ps1 = {}
 
             def first_mm(half, chunks):
@@ -185,7 +187,7 @@ def tile_causalexpert_pa_t_kernel(tc, x_attn, cw1, cb1, cw2, cb2, cln_g, cln_b, 
                             )
 
             regroup1("v", 0)
-            regroup1("s", 1)
+            regroup1("v", 1)
             nc.vector.quantize_mx(out=xq[:].bitcast(FP8X4), scales=xs[:], in_=xg[:])
             quant1(0)
             sm_ps = psum.tile([P, P], BF16, name="sm_ps", tag="pa1")
@@ -197,12 +199,13 @@ def tile_causalexpert_pa_t_kernel(tc, x_attn, cw1, cb1, cw2, cb2, cln_g, cln_b, 
             for hf in range(2):
                 cb_ps.append(psum.tile([P, 512], F32, name="cb_ps%d" % hf, tag="p%s1" % "ab"[hf]))
                 nc.tensor.matmul(cb_ps[hf][:], lhsT=pick[:], rhs=rows[:, 512 * hf : 512 * hf + 512], start=True, stop=True)
-            regroup1("v", 2)
             quant1(1)
             first_mm(0, range(4))
+            regroup1("s", 2)
+            regroup1("v", 3, 0, 256)
+            regroup1("s", 3, 256, 512)
             quant1(2)
             for c0 in (0, 256):
-                regroup1("s", 3, c0, c0 + 256)
                 quant1(3, c0, c0 + 256)
                 first_mm(1, range(c0 // 128, c0 // 128 + 2))
             for hf in range(2):
@@ -218,7 +221,6 @@ def tile_causalexpert_pa_t_kernel(tc, x_attn, cw1, cb1, cw2, cb2, cln_g, cln_b, 
                 part = src4[:, :, 0:16, :][:, :, ::-1, :] if lo else src4[:, :, 16:32, :]
                 nc.vector.tensor_tensor(out=a_pos[:, 4 * h : 4 * h + 4, 16 * lo : 16 * lo + 16, :], in0=part, in1=bias, op=ALU.add)
         e_ps = [ps1[(1, h)][:].rearrange("p t (b i) -> p b i t", b=4) for h in range(2)]
-        e4 = eT[:].rearrange("p (b i) t -> p b i t", b=B)
 
         ssum = const.tile([P, 2 * N_TILES], F32, name="ssum")
         nm = const.tile([P, N_TILES], F32, name="nm")
@@ -243,10 +245,12 @@ def tile_causalexpert_pa_t_kernel(tc, x_attn, cw1, cb1, cw2, cb2, cln_g, cln_b, 
                 w, parts = tiles[t0 + ti]
                 for s0, ns, j in parts:
                     if t0 + ti in G_ADDS:
+                        k, n4 = (0, j - 3) if j < 16 else (1, j - 17)
+                        assert n4 % 4 == 0
                         nc.gpsimd.tensor_tensor(
                             out=view[:, :, s0 : s0 + ns, :],
                             in0=a_pos[:, :, w + s0 : w + s0 + ns, :],
-                            in1=e4[:, :, j : j + 1, :].to_broadcast([P, B, ns, 4]),
+                            in1=eT[:, k, :, n4 // 4 : n4 // 4 + 1, :].to_broadcast([P, B, ns, 4]),
                             op=ALU.add,
                         )
                     else:
@@ -335,7 +339,7 @@ def tile_causalexpert_pa_t_kernel(tc, x_attn, cw1, cb1, cw2, cb2, cln_g, cln_b, 
         back = {}
 
         def stage_empty():
-            for half in range(2):
+            for half in (1, 0):
                 for key in range(2):
                     gain = smT[:, 2 * key : 2 * key + 2].unsqueeze(2).unsqueeze(3).to_broadcast([P, 2, B, 16])
                     src = acc[key][:, :, :, 16 * half : 16 * half + 16]
@@ -382,7 +386,8 @@ def tile_causalexpert_pa_t_kernel(tc, x_attn, cw1, cb1, cw2, cb2, cln_g, cln_b, 
                 queue.dma_start(out=out[b, i0 : i0 + 16, :], in_=osb[16 * b : 16 * b + 16, :])
 
         for h in range(2):
-            nc.scalar.copy(out=eT[:, 128 * h : 128 * h + 128, :], in_=ps1[(1, h)][:].rearrange("p t r -> p r t"))
+            for k in range(2):
+                nc.scalar.copy(out=eT[:, k, 4 * h : 4 * h + 4, :, :], in_=e_ps[h][:, :, 3 + 14 * k : 16 + 14 * k : 4, :])
         stage_add(0)
         stage_add(1)
         stage_gelu(0)
@@ -440,7 +445,7 @@ def tile_causalexpert_pa_t_kernel(tc, x_attn, cw1, cb1, cw2, cb2, cln_g, cln_b, 
         for t in (last - 2, last - 1):
             stage_sum(t)
         stage_empty()
-        back_add("H")
         back_add("L")
-        stage_store("H")
+        back_add("H")
         stage_store("L")
+        stage_store("H")

from contextlib import ExitStack

import concourse.mybir as mybir
from concourse.masks import make_identity

F32 = mybir.dt.float32
BF16 = mybir.dt.bfloat16
U32 = mybir.dt.uint32
U8 = mybir.dt.uint8
I32 = mybir.dt.int32
FP8X4 = mybir.dt.float8_e4m3fn_x4
ALU = mybir.AluOpType
ACT = mybir.ActivationFunctionType

P = 128
B, L, D, C = 8, 32, 1024, 512
EPS = 1e-5
FLOPS = 2 * (B * L) * (2 * D) * C + 2 * (B * L * (L + 1) // 2) * C * D

N_TILES = 33
GROUPS = [1, 2, 2] + [4] * 7
QUANTS = [(0, 1), (1, 8), (9, 8), (17, 8), (25, 8)]
G_ADDS = (8, 12, 16, 19, 23)


def z_engines(t):
    return "v" if t > N_TILES - 5 else "g"


def tile_parts():
    tiles = [(0, [(0, 16, 0)]), (16, [(0, 16, 0)])]
    for w in range(15, 0, -1):
        tiles.append((w, [(0, 16 - w, 16 + w), (16 - w, w, 16 - w)]))
    for n in range(1, 17):
        tiles.append((0, [(0, 16, n)]))
    return tiles


def tile_causalexpert_pa_t_kernel(tc, x_attn, cw1, cb1, cw2, cb2, cln_g, cln_b, out):
    nc = tc.nc
    tiles = tile_parts()
    groups = []
    t0 = 0
    for n in GROUPS:
        groups.append((t0, n))
        t0 += n
    n_groups = len(groups)
    group_of = {}
    for g in range(n_groups):
        for t in range(groups[g][0], groups[g][0] + groups[g][1]):
            group_of[t] = g

    with ExitStack() as ctx:
        const = ctx.enter_context(tc.tile_pool(name="const", bufs=1))
        hp_pool = ctx.enter_context(tc.tile_pool(name="hp", bufs=4))
        junk_pool = ctx.enter_context(tc.tile_pool(name="junk", bufs=2))
        psum = ctx.enter_context(tc.psum_pool(name="psum", bufs=1))
        ctx.enter_context(tc.manual_schedule())

        w2_pool = ctx.enter_context(tc.tile_pool(name="w2", bufs=1))
        with tc.tile_pool(name="head", bufs=1) as head:
            x_sb = head.tile([P, 2048], BF16, name="x_sb")
            raw1 = head.tile([P, 4, 2048], BF16, name="raw1")
            w1_view = cw1.rearrange("(g p j) c -> p g (j c)", g=4, p=P, j=4)
            nc.sync.dma_start(out=raw1[:, 0, :], in_=w1_view[:, 0, :])
            nc.sync.dma_start(
                out=x_sb[:].rearrange("p (h d) -> p h d", h=2),
                in_=x_attn.flatten_outer_dims().rearrange("(h p) d -> p h d", p=P),
            )
            nc.sync.dma_start(out=raw1[:, 1, :], in_=w1_view[:, 1, :])
            nc.sync.dma_start(out=raw1[:, 2, :], in_=w1_view[:, 2, :])
            nc.sync.dma_start(out=raw1[:, 3, :], in_=w1_view[:, 3, :])
            raw2 = w2_pool.tile([P, 4, 1024], BF16, name="raw2")
            w2_view = cw2.rearrange("(t p) n -> p t n", p=P)
            for hf in range(2):
                nc.sync.dma_start(out=raw2[:, :, 512 * hf : 512 * hf + 512], in_=w2_view[:, :, 512 * hf : 512 * hf + 512])

            ident_f = const.tile([P, P], F32, name="ident_f")
            make_identity(nc, ident_f[:])
            sm = const.tile([P, P], BF16, name="sm")
            nc.vector.memset(sm[:], 0.0)
            rows = const.tile([P, 1024], BF16, name="rows")
            nc.vector.memset(rows[:], 0.0)
            nc.scalar.dma_start(out=sm[0:8, :], in_=cln_g.rearrange("(c p) -> c p", p=P))
            nc.scalar.dma_start(out=sm[8:12, :], in_=cb1.rearrange("(t p) -> t p", p=P))
            nc.scalar.dma_start(out=rows[0:1, :], in_=cln_b.rearrange("(o n) -> o n", o=1))
            nc.scalar.dma_start(out=rows[32:33, :], in_=cb2.rearrange("(o n) -> o n", o=1))
            warm = const.tile([P, 2], F32, name="warm")
            nc.vector.memset(warm[:], 0.0)
            warm_o = const.tile([P, 2], BF16, name="warm_o")
            nc.scalar.activation(out=warm_o[:], in_=warm[:], func=ACT.Gelu)
            ident_b = const.tile([P, P], BF16, name="ident_b")
            nc.vector.tensor_copy(out=ident_b[:], in_=ident_f[:])
            pick = const.tile([P, P], BF16, name="pick")
            nc.vector.memset(pick[:], 0.0)
            nc.vector.memset(pick[32:33, :], 1.0)
            deps = const.tile([P, 1], F32, name="deps")
            nc.vector.tensor_scalar(out=deps[:], in0=warm[:, 0:1], scalar1=1.0, scalar2=D * EPS, op0=ALU.mult, op1=ALU.add)
            cnt = {}
            for a, base in (("H", 17), ("L", 1)):
                cnt_i = const.tile([P, P], I32, name="cnt_i" + a)
                nc.gpsimd.iota(cnt_i[:], pattern=[[0, B], [1, 16]], base=base, channel_multiplier=0)
                cnt[a] = const.tile([P, P], BF16, name="cnt" + a)
                nc.vector.memset(cnt[a][:], 0.0)
                nc.vector.tensor_scalar(out=cnt[a][0:1, :], in0=cnt_i[0:1, :], scalar1=1.0 / 32.0, scalar2=None, op0=ALU.mult)

            xw = x_sb[:].bitcast(F32)
            xg = head.tile([P, 2048], BF16, name="xg", align_bytes=64)
            xgw = xg[:].bitcast(F32)
            for g in range(2):
                xt = psum.tile([P, 2, 2, P], F32, name="xt%d" % g, tag="p%s0" % "ab"[g])
                for h in range(2):
                    for u in range(2):
                        col = 512 * h + 256 * g
                        nc.tensor.transpose(xt[:, h, u, :], xw[:, col + u : col + 256 : 2], ident_f[:])
                dst = xgw[:, 512 * g : 512 * g + 512].rearrange("p (h r u) -> p h r u", h=2, u=2)
                src = xt[:].rearrange("p h u r -> p h r u")
                nc.scalar.copy(out=dst, in_=src)
            xq = head.tile([P, 512], U32, name="xq", align_bytes=64)
            xs = head.tile([P, 512], U8, name="xs", align_bytes=64)

            def regroup(engine, dst, src):
                d = dst.rearrange("p (c i) t -> p c t i", i=4)
                s = src.rearrange("p t (c i) -> p c t i", i=4)
                if engine == "v":
                    nc.vector.tensor_copy(out=d, in_=s)
                else:
                    nc.scalar.copy(out=d, in_=s)

            w1q = head.tile([P, 2048], U32, name="w1q", align_bytes=64)
            w1s = head.tile([P, 2048], U8, name="w1s", align_bytes=64)
            w1g = [head.tile([P, 512, 4], BF16, name="w1g%d" % unit, align_bytes=64) for unit in range(4)]
            w2q = const.tile([P, 1024], U32, name="w2q", align_bytes=64)
            w2s = const.tile([P, 1024], U8, name="w2s", align_bytes=64)
            w2g = [w2_pool.tile([P, 512, 4], BF16, name="w2g%d" % hf, align_bytes=64) for hf in range(2)]

            def regroup2(hf):
                for k in range(4):
                    col = 512 * hf + 128 * k
                    nc.gpsimd.tensor_scalar(
                        out=w2g[hf][:, 128 * k : 128 * k + 128, :].rearrange("p (c i) t -> p c t i", i=4),
                        in0=raw2[:, :, col : col + 128].rearrange("p t (c i) -> p c t i", i=4),
                        scalar1=1.0,
                        scalar2=0.0,
                        op0=ALU.mult,
                        op1=ALU.add,
                    )

            def regroup1(engine, unit, c0=0, c1=512):
                src = raw1[:, unit, :].rearrange("p (j c) -> p j c", j=4)
                regroup(engine, w1g[unit][:, c0:c1, :], src[:, :, c0:c1])

            def quant1(unit, c0=0, c1=512):
                nc.vector.quantize_mx(
                    out=w1q[:, 512 * unit + c0 : 512 * unit + c1].bitcast(FP8X4),
                    scales=w1s[:, 512 * unit + c0 : 512 * unit + c1],
                    in_=w1g[unit][:, c0:c1, :].rearrange("p c t -> p (c t)"),
                )

            def quant2(hf):
                nc.vector.quantize_mx(
                    out=w2q[:, 512 * hf : 512 * hf + 512].bitcast(FP8X4),
                    scales=w2s[:, 512 * hf : 512 * hf + 512],
                    in_=w2g[hf][:].rearrange("p c t -> p (c t)"),
                )

            a_pos = const.tile([P, B, 32, 4], F32, name="a_pos")
            eT = const.tile([P, 2, B, 4, 4], F32, name="eT")
            ps1 = {}

            def first_mm(half, chunks):
                for t2 in chunks:
                    for h in range(2):
                        if t2 == 0:
                            ps1[(half, h)] = psum.tile([P, 4, P], F32, name="ps1_%d%d" % (half, h), tag="ye"[half] + str(h))
                        for g in range(2):
                            wc = 512 * (2 * half + g) + 128 * t2
                            xc = 256 * g + 128 * h
                            nc.tensor.matmul_mx(
                                out=ps1[(half, h)][:, t2, :],
                                lhsT=w1q[:, wc : wc + 128].bitcast(FP8X4),
                                lhsT_scale=w1s[:, wc : wc + 128],
                                rhs=xq[:, xc : xc + 128].bitcast(FP8X4),
                                rhs_scale=xs[:, xc : xc + 128],
                                start=(g == 0),
                                stop=(g == 1),
                            )

            regroup1("v", 0)
            regroup1("v", 1)
            nc.vector.quantize_mx(out=xq[:].bitcast(FP8X4), scales=xs[:], in_=xg[:])
            quant1(0)
            sm_ps = psum.tile([P, P], BF16, name="sm_ps", tag="pa1")
            nc.tensor.transpose(sm_ps[:], sm[:], ident_b[:])
            smT = const.tile([P, 12], F32, name="smT")
            nc.vector.tensor_copy(out=smT[:], in_=sm_ps[:, 0:12])
            cb2_bc = const.tile([P, 1024], F32, name="cb2_bc")
            cb_ps = []
            for hf in range(2):
                cb_ps.append(psum.tile([P, 512], F32, name="cb_ps%d" % hf, tag="p%s1" % "ab"[hf]))
                nc.tensor.matmul(cb_ps[hf][:], lhsT=pick[:], rhs=rows[:, 512 * hf : 512 * hf + 512], start=True, stop=True)
            quant1(1)
            first_mm(0, range(4))
            regroup1("s", 2)
            regroup1("v", 3, 0, 256)
            regroup1("s", 3, 256, 512)
            quant1(2)
            for c0 in (0, 256):
                quant1(3, c0, c0 + 256)
                first_mm(1, range(c0 // 128, c0 // 128 + 2))
            for hf in range(2):
                nc.scalar.copy(out=cb2_bc[:, 512 * hf : 512 * hf + 512], in_=cb_ps[hf][:])
            nc.vector.memset(w2g[0][:, 0:1, :], 0.0)
            regroup2(0)
        y_pool = ctx.enter_context(tc.tile_pool(name="y", bufs=8))
        z_pool = ctx.enter_context(tc.tile_pool(name="z", bufs=8))
        bias = smT[:, 8:12].unsqueeze(1).unsqueeze(1).to_broadcast([P, 4, 16, 4])
        for lo in range(2):
            for h in range(2):
                src4 = ps1[(0, h)][:].rearrange("p t (b i) -> p b i t", b=4)
                part = src4[:, :, 0:16, :][:, :, ::-1, :] if lo else src4[:, :, 16:32, :]
                nc.vector.tensor_tensor(out=a_pos[:, 4 * h : 4 * h + 4, 16 * lo : 16 * lo + 16, :], in0=part, in1=bias, op=ALU.add)
        e_ps = [ps1[(1, h)][:].rearrange("p t (b i) -> p b i t", b=4) for h in range(2)]

        ssum = const.tile([P, 2 * N_TILES], F32, name="ssum")
        nm = const.tile([P, N_TILES], F32, name="nm")
        ssq = const.tile([P, N_TILES], F32, name="ssq")
        wv = const.tile([P, N_TILES], F32, name="wv")
        hq = const.tile([P, P * N_TILES], U32, name="hq", align_bytes=64)
        hs = const.tile([P, P * N_TILES], U8, name="hs", align_bytes=64)
        h2 = const.tile([P, 512 * N_TILES], BF16, name="h2", align_bytes=64)

        acc = {}
        hp_t = {}
        yps_t = {}
        y_t = {}
        z_t = {}
        ident3 = ident_f[:].rearrange("p (b s) -> p b s", b=B)

        def stage_add(g):
            t0, n = groups[g]
            hp_t[g] = hp_pool.tile([P, 2048], F32, name="hp")
            for ti in range(n):
                view = hp_t[g][:, 512 * ti : 512 * ti + 512].rearrange("p (b s t) -> p b s t", b=B, t=4)
                w, parts = tiles[t0 + ti]
                for s0, ns, j in parts:
                    if t0 + ti in G_ADDS:
                        k, n4 = (0, j - 3) if j < 16 else (1, j - 17)
                        assert n4 % 4 == 0
                        nc.gpsimd.tensor_tensor(
                            out=view[:, :, s0 : s0 + ns, :],
                            in0=a_pos[:, :, w + s0 : w + s0 + ns, :],
                            in1=eT[:, k, :, n4 // 4 : n4 // 4 + 1, :].to_broadcast([P, B, ns, 4]),
                            op=ALU.add,
                        )
                    else:
                        for h in range(2):
                            nc.vector.tensor_tensor(
                                out=view[:, 4 * h : 4 * h + 4, s0 : s0 + ns, :],
                                in0=a_pos[:, 4 * h : 4 * h + 4, w + s0 : w + s0 + ns, :],
                                in1=e_ps[h][:, :, j : j + 1, :].to_broadcast([P, 4, ns, 4]),
                                op=ALU.add,
                            )

        def stage_gelu(g):
            t0, n = groups[g]
            nc.scalar.activation(out=h2[:, 512 * t0 : 512 * (t0 + n)], in_=hp_t[g][:, 0 : 512 * n], func=ACT.Gelu)

        def stage_quant(k):
            first, count = QUANTS[k]
            sl = slice(P * first, P * (first + count))
            nc.vector.quantize_mx(out=hq[:, sl].bitcast(FP8X4), scales=hs[:, sl], in_=h2[:, 512 * first : 512 * (first + count)])

        def stage_mm(t):
            for hf in range(2):
                yps_t[(t, hf)] = psum.tile([P, 512], F32, name="yps", tag="ye"[t % 2] + str(hf))
                nc.tensor.matmul_mx(
                    out=yps_t[(t, hf)][:],
                    lhsT=hq[:, P * t : P * t + P].bitcast(FP8X4),
                    lhsT_scale=hs[:, P * t : P * t + P],
                    rhs=w2q[:, 512 * hf : 512 * hf + 512].bitcast(FP8X4),
                    rhs_scale=w2s[:, 512 * hf : 512 * hf + 512],
                    start=True,
                    stop=True,
                )

        def stage_bias(t):
            y_t[t] = y_pool.tile([P, 1024], F32, name="y")
            for hf in range(2):
                nc.vector.scalar_tensor_tensor(
                    out=y_t[t][:, 512 * hf : 512 * hf + 512],
                    in0=yps_t[(t, hf)][:],
                    scalar=1.0,
                    in1=cb2_bc[:, 512 * hf : 512 * hf + 512],
                    op0=ALU.mult,
                    op1=ALU.add,
                    accum_out=ssum[:, 2 * t + hf : 2 * t + hf + 1],
                )

        def stage_nm(t):
            scaled = junk_pool.tile([P, 2], F32, name="scaled")
            nc.scalar.activation(out=scaled[:], in_=ssum[:, 2 * t : 2 * t + 2], func=ACT.Identity, scale=-1.0 / D, accum_out=nm[:, t : t + 1])

        def stage_square(t):
            junk = junk_pool.tile([P, 1024], BF16, name="junk")
            nc.scalar.activation(out=junk[:], in_=y_t[t][:], func=ACT.Square, bias=nm[:, t : t + 1], scale=1.0, accum_out=ssq[:, t : t + 1])

        def stage_weight(t, n):
            sl = slice(t, t + n)
            nc.scalar.activation(out=wv[:, sl], in_=ssq[:, sl], func=ACT.Abs_reciprocal_sqrt, bias=deps[:], scale=1.0)

        def stage_z(t):
            z_t[t] = z_pool.tile([P, 1024], F32, name="z")
            eng = z_engines(t)
            wd = 1024 // len(eng)
            for k in range(len(eng)):
                sl = slice(wd * k, wd * k + wd)
                engine = nc.gpsimd if eng[k] == "g" else nc.vector
                engine.tensor_scalar(
                    out=z_t[t][:, sl], in0=y_t[t][:, sl], scalar1=nm[:, t : t + 1], scalar2=wv[:, t : t + 1], op0=ALU.add, op1=ALU.mult
                )

        def stage_sum(t):
            w = tiles[t][0]
            for c in range(8):
                key = c // 2
                if key not in acc:
                    acc[key] = psum.tile([P, 2, B, 32], F32, name="acc%d" % key, tag="p%s%d" % ("ab"[c // 4], key % 2))
                nc.tensor.matmul(
                    acc[key][:, c % 2, :, w : w + 16],
                    lhsT=z_t[t][:, 128 * c : 128 * c + 128],
                    rhs=ident3,
                    is_transpose=True,
                    start=(t == 0 and c % 2 == 0),
                    stop=(t == N_TILES - 2 and c % 2 == 1),
                )

        oT = const.tile([P, 2, 8, B, 16], F32, name="oT")
        back = {}

        def stage_empty():
            for half in (1, 0):
                for key in range(2):
                    gain = smT[:, 2 * key : 2 * key + 2].unsqueeze(2).unsqueeze(3).to_broadcast([P, 2, B, 16])
                    src = acc[key][:, :, :, 16 * half : 16 * half + 16]
                    nc.vector.tensor_tensor(
                        out=oT[:, half, 2 * key : 2 * key + 2, :, :], in0=src[:, :, :, ::-1] if half else src, in1=gain, op=ALU.mult
                    )
                for c in range(4, 8):
                    src = acc[c // 2][:, c % 2, :, 16 * half : 16 * half + 16]
                    nc.scalar.activation(
                        out=oT[:, half, c, :, :], in_=src[:, :, ::-1] if half else src, func=ACT.Copy, scale=smT[:, c : c + 1]
                    )

        def back_open(a):
            for hb in range(2):
                back[(a, hb)] = psum.tile([P, 512], F32, name="back%s%d" % (a, hb), tag=("e" if a == "H" else "y") + str(hb))
                nc.tensor.matmul(back[(a, hb)][:], lhsT=cnt[a][:], rhs=rows[:, 512 * hb : 512 * hb + 512], start=True, stop=False)

        def back_add(a):
            for hb in range(2):
                for c in range(4):
                    nc.tensor.matmul(
                        back[(a, hb)][:, 128 * c : 128 * c + 128],
                        lhsT=oT[:, "HL".index(a), 4 * hb + c, :, :].rearrange("p b s -> p (b s)"),
                        rhs=ident_f[:],
                        is_transpose=True,
                        start=False,
                        stop=(c == 3),
                    )

        def stage_store(a):
            osb = const.tile([P, 1024], F32, name="osb" + a)
            for hb in range(2):
                cols = slice(512 * hb, 512 * hb + 512)
                if a == "H":
                    nc.vector.scalar_tensor_tensor(
                        out=osb[:, cols], in0=yg[:, cols], scalar=wv[:, N_TILES - 1 :], in1=back[(a, hb)][:], op0=ALU.mult, op1=ALU.add
                    )
                elif hb == 0:
                    nc.scalar.copy(out=osb[:, cols], in_=back[(a, hb)][:])
                else:
                    nc.vector.tensor_copy(out=osb[:, cols], in_=back[(a, hb)][:])
            queue, i0 = (nc.sync, 16) if a == "H" else (nc.scalar, 0)
            for b in range(B):
                queue.dma_start(out=out[b, i0 : i0 + 16, :], in_=osb[16 * b : 16 * b + 16, :])

        for h in range(2):
            for k in range(2):
                nc.scalar.copy(out=eT[:, k, 4 * h : 4 * h + 4, :, :], in_=e_ps[h][:, :, 3 + 14 * k : 16 + 14 * k : 4, :])
        stage_add(0)
        stage_add(1)
        stage_gelu(0)
        for g in range(2, n_groups):
            stage_add(g)
            if g == 8:
                regroup2(1)
            stage_gelu(g - 1)
        stage_gelu(n_groups - 1)
        quant2(0)
        quant2(1)
        nc.scalar.activation(out=warm_o[:], in_=warm[:], func=ACT.Abs_reciprocal_sqrt, bias=deps[:], scale=1.0)
        for k in range(2):
            stage_quant(k)
        g_bc = const.tile([P, 1024], BF16, name="g_bc")
        nc.vector.memset(g_bc[:, 0:2], 0.0)
        nc.sync.dma_start(out=g_bc[:], in_=cln_g.partition_broadcast(P))
        stage_mm(0)
        stage_mm(1)

        last = N_TILES - 1
        yg = const.tile([P, 1024], F32, name="yg")
        weights_at = {2: [(0, 1)], 3: [(1, 1)]}
        for t in range(2, last - 2, 2):
            weights_at.setdefault(t + 3, []).append((t, 2))
        sums_at = {t + 5: (t, t + 1) for t in range(0, 16, 2)}
        sums_at.update({4: (0,), 5: (1,)})
        sums_at.update({t + 5: (t, t + 1) for t in range(16, 28, 2)})
        for step in range(last + 1):
            stage_bias(step)
            stage_nm(step)
            for t, n in weights_at.get(step, []):
                stage_weight(t, n)
            if step >= 1:
                stage_square(step - 1)
            if step >= last - 1:
                stage_weight(step - 1, 1)
            if step in (0, 1, 2):
                stage_quant(2 + step)
            if step + 2 <= last:
                stage_mm(step + 2)
            if step >= 3:
                stage_z(step - 3)
            for t in sums_at.get(step, ()):
                stage_sum(t)
        stage_square(last)
        stage_weight(last, 1)
        stage_z(last - 2)
        nc.vector.scalar_tensor_tensor(out=yg[:], in0=y_t[last][:], scalar=nm[:, last:], in1=g_bc[:], op0=ALU.add, op1=ALU.mult)
        stage_z(last - 1)
        back_open("H")
        for t in (last - 4, last - 3):
            stage_sum(t)
        back_open("L")
        for t in (last - 2, last - 1):
            stage_sum(t)
        stage_empty()
        back_add("L")
        back_add("H")
        stage_store("L")
        stage_store("H")
